import numpy as np
import ml_dtypes


def mxq(x, axis, fmt="e4m3"):
    dtype, down = {"e4m3": (ml_dtypes.float8_e4m3fn, 7), "e5m2": (ml_dtypes.float8_e5m2, 14)}[fmt]
    v = np.moveaxis(np.asarray(x, np.float32).astype(ml_dtypes.bfloat16).astype(np.float64), axis, -1)
    blocks = v.reshape(v.shape[:-1] + (-1, 32))
    amax = np.abs(blocks).max(-1, keepdims=True)
    byte = np.maximum(np.where(amax > 0, np.frexp(amax)[1] - 1 + 127, 0) - down, 1)
    scale = np.exp2(byte - 127.0)
    codes = (blocks / scale).astype(np.float32).astype(dtype).astype(np.float64)
    return np.moveaxis((codes * scale).reshape(v.shape), -1, axis)


WIDE = False


def mx_kscale(k):
    if not WIDE:
        return np.ones(k)
    levels = np.array([10, -10, 5, -5, 0])
    a = np.random.permutation(np.resize(levels, k // 512 * 4)).reshape(k // 512, 4)
    idx = np.arange(k)
    return np.exp2(a[idx // 512, idx % 128 // 32])


BF16 = ml_dtypes.bfloat16


def bf(x):
    return np.asarray(x, np.float32).astype(BF16)


def f64(x):
    return np.asarray(x).astype(np.float64)


B, C, H, W = 4, 192, 64, 64
K = H * W
OFFSETS = [(-1, -1), (-1, 0), (-1, 1), (0, -1), (0, 0)]
EPS = 1e-12


def setup_inputs():
    s = mx_kscale(K)
    t = 2.0 ** np.round(np.log2(s.max() / s.min()) / 2)
    r = np.where(np.arange(H) % 2 == 0, 1.0 / t, t)
    return {"x": bf(np.random.standard_normal((B, C, H, W)) * r[None, None, :, None])}


def reference(x):
    x = f64(x)
    xp = np.pad(x, ((0, 0), (0, 0), (1, 1), (1, 1)), mode="edge")
    center = x.reshape(B, C, K).transpose(0, 2, 1)
    cq = mxq(center, 1, "e4m3")
    cofe = []
    for dy, dx in OFFSETS:
        if (dy, dx) == (0, 0):
            sq = cq
        else:
            side = xp[:, :, 1 + dy:1 + dy + H, 1 + dx:1 + dx + W].reshape(B, C, K).transpose(0, 2, 1)
            sq = mxq(side, 1, "e4m3")
        co = cq.transpose(0, 2, 1) @ sq
        cofe.append(co.reshape(B, C * C))
    cofe = np.stack(cofe, axis=1)
    norm = np.sqrt((cofe ** 2).sum(-1, keepdims=True))
    return cofe / np.maximum(norm, EPS)

@@ -1,0 +1,336 @@
+from contextlib import ExitStack
+
+import concourse.mybir as mybir
+from concourse.masks import make_identity
+
+F32 = mybir.dt.float32
+BF16 = mybir.dt.bfloat16
+U32 = mybir.dt.uint32
+I32 = mybir.dt.int32
+U8 = mybir.dt.uint8
+FP8X4 = mybir.dt.float8_e4m3fn_x4
+
+B, C, H, W = 4, 192, 64, 64
+K = H * W
+OFFSETS = 5
+EPS = 1e-12
+FLOPS = 2 * B * OFFSETS * C * C * K
+
+P = 128
+ROW_TILES = B * C // P
+CLASSES = 8
+ROW_BLOCKS = CLASSES + 1
+LEFT, MID, RIGHT = 0, 1, 2
+MAPS = 3
+BLOCK_COLS = MAPS * C
+N_MOVE = 512
+TAIL = C - P
+CODE_COLS = BLOCK_COLS * CLASSES + N_MOVE + P
+TAIL_COLS = (ROW_BLOCKS + 1) * TAIL
+SLOTS = 9
+SLOT_WORDS = 16
+SORTED_CLASSES = 4
+SORTED = 2 * SORTED_CLASSES * SLOTS * 2 * SLOT_WORDS
+PAD = 16
+BLOCK_ORDER = [1, 2, 3, 4, 5, 6, 7, 8, 0]
+FIRST_CLASS, LAST_CLASS = 1, 0
+SORTS_IN_TWO_ROUNDS = 3
+LAG = 2
+FINISH_ROUNDS = 8
+
+
+def tiles_of(b):
+    first = 3 * (b // 2)
+    return [first, first + 1] if b % 2 == 0 else [first + 2]
+
+
+def batch_pieces(t):
+    b, c0 = divmod(t * P, C)
+    rows = min(P, C - c0)
+    pieces = [(b, c0, 0, rows)]
+    if rows < P:
+        pieces.append((b + 1, 0, rows, P - rows))
+    return pieces
+
+
+def tile_cofeature_fast_pa_kernel(tc, x, out):
+    nc = tc.nc
+    x_rows = x.rearrange("b c i j -> (b c) (i j)")
+
+    with ExitStack() as ctx:
+        const = ctx.enter_context(tc.tile_pool(name="const", bufs=1))
+        sorted_pool = ctx.enter_context(tc.tile_pool(name="sorted", bufs=3))
+        stage_pool = ctx.enter_context(tc.tile_pool(name="stage", bufs=6))
+        result_pool = ctx.enter_context(tc.tile_pool(name="result", bufs=2))
+        small_pool = ctx.enter_context(tc.tile_pool(name="small", bufs=2))
+        flip_pool = ctx.enter_context(tc.psum_pool(name="flip", bufs=4))
+        acc_pool = ctx.enter_context(tc.psum_pool(name="acc", bufs=1))
+
+        ident = const.tile([P, P], F32)
+        make_identity(nc, ident[:])
+        all_rows = const.tile([P, P], F32)
+        nc.vector.memset(all_rows[:], 1.0)
+        upper_rows = const.tile([P, P], F32)
+        nc.vector.memset(upper_rows[0:64, :], 0.0)
+        nc.vector.memset(upper_rows[64:P, :], 1.0)
+        lower_rows = const.tile([P, P], F32)
+        nc.vector.memset(lower_rows[0:64, :], 1.0)
+        nc.vector.memset(lower_rows[64:P, :], 0.0)
+        warm = const.tile([P, 1], F32)
+        nc.vector.memset(warm[:], 1.0)
+        nc.scalar.sqrt(out=warm[:], in_=warm[:])
+        squares = const.tile([P, C], F32)
+
+        plain_tiles = [const.tile([P, PAD + K + PAD], BF16, name="plain%d" % i) for i in range(3)]
+        for plain in plain_tiles:
+            nc.vector.memset(plain[:, 0:PAD], 0.0)
+            nc.vector.memset(plain[:, PAD + K :], 0.0)
+
+        sorted_tiles = {}
+        codes = {}
+        scales = {}
+        tail_codes = {}
+        tail_scales = {}
+        acc = {}
+
+        def load(t):
+            nc.sync.dma_start(out=plain_tiles[t % 3][:, PAD : PAD + K], in_=x_rows[t * P : (t + 1) * P, :])
+
+        def sort_rows(t, m, part):
+            plain = plain_tiles[t % 3]
+            shift = m - MID
+            by_class = plain[:, PAD + shift : PAD + shift + K].rearrange(
+                "p (s g e u r) -> p g s e u r", s=8, g=CLASSES, e=2, u=2, r=16
+            )
+            mine = slice(SORTED_CLASSES * part, SORTED_CLASSES * (part + 1))
+            tidy = sorted_pool.tile([P, SORTED], BF16, tag="sorted%d%d" % (m, part))
+            view = tidy[:].rearrange("p (u g s e r) -> p u g s e r", u=2, g=SORTED_CLASSES, s=SLOTS, e=2, r=16)
+            nc.vector.tensor_copy(
+                out=view[:, :, :, 1:SLOTS].rearrange("p u g s e r -> p g s e u r"), in_=by_class[:, mine]
+            )
+            edge = plain[:, PAD : PAD + K].rearrange("p (s g j) -> p g s j", s=8, g=CLASSES, j=W)
+            if m == LEFT:
+                nc.gpsimd.tensor_copy(out=view[:, 0, :, 1:SLOTS, 0, 0:1], in_=edge[:, mine, :, 0:1])
+            if m == RIGHT:
+                nc.gpsimd.tensor_copy(out=view[:, 1, :, 1:SLOTS, 1, 15:16], in_=edge[:, mine, :, W - 1 : W])
+            if part == 1:
+                first_part = sorted_tiles[(t, m, 0)][:].rearrange(
+                    "p (u g s e r) -> p u g s e r", u=2, g=SORTED_CLASSES, s=SLOTS, e=2, r=16
+                )
+                nc.gpsimd.tensor_copy(out=view[:, :, SORTED_CLASSES - 1, 0], in_=first_part[:, :, 0, 1])
+            sorted_tiles[(t, m, part)] = tidy
+
+        def block_words(t, m, u, h):
+            g, first_slot = (CLASSES - 1, 0) if h == 0 else (h - 1, 1)
+            part, g_in_part = divmod(g, SORTED_CLASSES)
+            start = ((u * SORTED_CLASSES + g_in_part) * SLOTS + first_slot) * SLOT_WORDS
+            return sorted_tiles[(t, m, part)][:].bitcast(F32)[:, start : start + P]
+
+        used = BLOCK_COLS * CLASSES + 2 * C
+        for i in range(3):
+            code_tile = const.tile([P, CODE_COLS], U32, name="codes%d" % i, align_bytes=64)
+            scale_tile = const.tile([P, CODE_COLS], U8, name="scales%d" % i, align_bytes=64)
+            nc.vector.memset(code_tile[:].bitcast(I32)[:, used:CODE_COLS], 0)
+            nc.vector.memset(scale_tile[:].bitcast(I32)[:, used // 4 : CODE_COLS // 4], 0)
+            tail_code_tile = const.tile([P, TAIL_COLS], U32, name="tail_codes%d" % i, align_bytes=64)
+            tail_scale_tile = const.tile([P, TAIL_COLS], U8, name="tail_scales%d" % i, align_bytes=64)
+            for first in (0, TAIL_COLS - TAIL):
+                nc.vector.memset(tail_code_tile[:].bitcast(I32)[:, first : first + TAIL], 0)
+                nc.vector.memset(tail_scale_tile[:].bitcast(I32)[:, first // 4 : (first + TAIL) // 4], 0)
+            for b in range(i, B, 3):
+                codes[b], scales[b] = code_tile, scale_tile
+                tail_codes[b], tail_scales[b] = tail_code_tile, tail_scale_tile
+
+        def banks_of(pairs):
+            banks = [[(t, LEFT, h), (t, MID, h)] for t, h in pairs]
+            right = [(t, RIGHT, h) for t, h in pairs if h < CLASSES]
+            return banks + [right] if right else banks
+
+        def transpose_step(pairs):
+            flipped_banks = []
+            for units in banks_of(pairs):
+                flipped = flip_pool.tile([P, 4 * P], F32, tag="flip")
+                for a, (t, m, h) in enumerate(units):
+                    for u in range(2):
+                        at = (2 * a + u) * P
+                        nc.tensor.transpose(flipped[:, at : at + P], block_words(t, m, u, h), ident[:])
+                flipped_banks.append(flipped)
+            return flipped_banks
+
+        def group_step(pairs, flipped_banks):
+            grouped_tiles = []
+            for units, flipped in zip(banks_of(pairs), flipped_banks):
+                words = 2 * P * len(units)
+                grouped = stage_pool.tile([P, 8 * P], BF16, tag="grouped", align_bytes=64)
+                nc.scalar.copy(
+                    out=grouped[:].bitcast(F32)[:, 0:words].rearrange("p (a n u) -> p a n u", a=len(units), u=2),
+                    in_=flipped[:, 0:words].rearrange("p (a u n) -> p a n u", a=len(units), u=2),
+                )
+                grouped_tiles.append(grouped)
+            return grouped_tiles
+
+        def quantise_step(pairs, grouped_tiles):
+            for units, grouped in zip(banks_of(pairs), grouped_tiles):
+                for a, (t, m, h) in enumerate(units):
+                    for b, c0, n0, rows in batch_pieces(t):
+                        col = BLOCK_COLS * h + C * m + c0
+                        at = 4 * (P * a + n0)
+                        nc.vector.quantize_mx(
+                            out=codes[b][:, col : col + rows].bitcast(FP8X4),
+                            scales=scales[b][:, col : col + rows],
+                            in_=grouped[:, at : at + 4 * rows],
+                        )
+                        if m == MID and h >= 1 and c0 + rows == C:
+                            at = 4 * (P * a + n0 + rows - TAIL)
+                            nc.vector.quantize_mx(
+                                out=tail_codes[b][:, TAIL * h : TAIL * (h + 1)].bitcast(FP8X4),
+                                scales=tail_scales[b][:, TAIL * h : TAIL * (h + 1)],
+                                in_=grouped[:, at : at + 4 * TAIL],
+                            )
+
+        def mx_pass(acc_tile, b, stationary, c_cols, d_cols, first, last):
+            stat_codes, stat_scales = stationary
+            nc.tensor.matmul_mx(
+                out=acc_tile,
+                lhsT=stat_codes[:, c_cols].bitcast(FP8X4),
+                lhsT_scale=stat_scales[:, c_cols],
+                rhs=codes[b][:, d_cols].bitcast(FP8X4),
+                rhs_scale=scales[b][:, d_cols],
+                start=first,
+                stop=last,
+            )
+
+        def multiply_class(b, g):
+            if g == FIRST_CLASS:
+                main0 = acc_pool.tile([P, N_MOVE], F32)
+                main1 = acc_pool.tile([P, N_MOVE], F32)
+                tail0 = acc_pool.tile([P, N_MOVE], F32)
+                tail1 = acc_pool.tile([P, N_MOVE], F32)
+                acc[b] = (main0, main1, tail0, tail1)
+            main0, main1, tail0, tail1 = acc[b]
+            c_first = BLOCK_COLS * (g + 1) + C * MID
+            d_first = BLOCK_COLS * g
+            for half, acc_tile in enumerate((main0, main1)):
+                mx_pass(
+                    acc_tile[:], b, (codes[b], scales[b]), slice(c_first, c_first + P),
+                    slice(d_first + N_MOVE * half, d_first + N_MOVE * (half + 1)), g == FIRST_CLASS, g == LAST_CLASS,
+                )
+            for h in [g] if g < CLASSES - 1 else [g, g + 1]:
+                c_cols = slice(TAIL * h, TAIL * h + P)
+                d_first = BLOCK_COLS * h
+                tail = (tail_codes[b], tail_scales[b])
+                first, last = h == FIRST_CLASS, h == LAST_CLASS
+                mx_pass(tail0[:], b, tail, c_cols, slice(d_first, d_first + N_MOVE), first, last)
+                mx_pass(tail1[:, 0:P], b, tail, c_cols, slice(d_first + N_MOVE, d_first + N_MOVE + P), first, last)
+
+        result = {}
+        sums = {}
+        inv = {}
+
+        def drain(b):
+            main0, main1, tail0, tail1 = acc[b]
+            g_main = result_pool.tile([P, OFFSETS * C], F32, tag="g_main")
+            nc.vector.tensor_copy(out=g_main[:, 0:N_MOVE], in_=main0[:])
+            nc.vector.tensor_copy(out=g_main[:, N_MOVE:], in_=main1[:, 0 : OFFSETS * C - N_MOVE])
+            g_tail = result_pool.tile([P, MAPS * C], F32, tag="g_tail")
+            nc.scalar.copy(out=g_tail[:, 0:N_MOVE], in_=tail0[:])
+            nc.scalar.copy(out=g_tail[:, N_MOVE:], in_=tail1[:, 0 : MAPS * C - N_MOVE])
+            result[b] = (g_main, g_tail)
+            sums_main = small_pool.tile([P, OFFSETS], F32, tag="sums_main")
+            sums_tail = small_pool.tile([P, MAPS], F32, tag="sums_tail")
+            sums[b] = (sums_main, sums_tail)
+
+        def square(b, o):
+            for g_sb, sums_sb in zip(result[b], sums[b]):
+                if C * o < g_sb.shape[1]:
+                    nc.scalar.activation(
+                        out=squares[:],
+                        in_=g_sb[:, C * o : C * (o + 1)],
+                        func=mybir.ActivationFunctionType.Square,
+                        accum_out=sums_sb[:, o : o + 1],
+                    )
+
+        def total_up(b):
+            sums_main, sums_tail = sums[b]
+            total = flip_pool.tile([P, 4 * P], F32, tag="flip")
+            nc.tensor.matmul(out=total[:, 0:OFFSETS], lhsT=all_rows[:], rhs=sums_main[:], start=True, stop=False)
+            nc.tensor.matmul(out=total[:, 0:MAPS], lhsT=upper_rows[:], rhs=sums_tail[:], start=False, stop=False)
+            nc.tensor.matmul(
+                out=total[:, MAPS:OFFSETS], lhsT=lower_rows[:], rhs=sums_tail[:, 0 : OFFSETS - MAPS], start=False, stop=True
+            )
+            inv_tile = small_pool.tile([P, OFFSETS], F32, tag="inv")
+            nc.vector.tensor_scalar_max(out=inv_tile[:], in0=total[:, 0:OFFSETS], scalar1=EPS * EPS)
+            nc.scalar.sqrt(out=inv_tile[:], in_=inv_tile[:])
+            inv[b] = inv_tile
+
+        def scale_and_store(b):
+            g_main, g_tail = result[b]
+            nc.vector.reciprocal(out=inv[b][:], in_=inv[b][:])
+            by_channel = out[b].rearrange("o (c d) -> c o d", d=C)
+            main_view = g_main[:].rearrange("p (o d) -> p o d", d=C)
+            nc.vector.tensor_tensor(
+                out=main_view,
+                in0=main_view,
+                in1=inv[b][:].unsqueeze(2).to_broadcast([P, OFFSETS, C]),
+                op=mybir.AluOpType.mult,
+            )
+            nc.sync.dma_start(out=by_channel[0:P], in_=main_view)
+            for rows, first_o, last_o in ((slice(64, P), 0, MAPS), (slice(0, 64), MAPS, OFFSETS)):
+                tail_view = g_tail[rows, 0 : C * (last_o - first_o)].rearrange("p (o d) -> p o d", d=C)
+                nc.gpsimd.tensor_tensor(
+                    out=tail_view,
+                    in0=tail_view,
+                    in1=inv[b][rows, first_o:last_o].unsqueeze(2).to_broadcast([64, last_o - first_o, C]),
+                    op=mybir.AluOpType.mult,
+                )
+                nc.sync.dma_start(out=by_channel[P:C, first_o:last_o], in_=tail_view)
+
+        steps = []
+        last_step = {}
+        sort_jobs = []
+        for b in range(B):
+            tiles = tiles_of(b)
+            blocks_a_step = 2 // len(tiles)
+            for first in range(0, ROW_BLOCKS, blocks_a_step):
+                blocks = BLOCK_ORDER[first : first + blocks_a_step]
+                classes = [h - 1 for h in blocks if h >= 2] + [0 for h in blocks if h == 0]
+                steps.append((b, first, [(t, h) for h in blocks for t in tiles], classes))
+            last_step[len(steps) - 1] = b
+            sort_jobs.extend([(t, m, part) for part in range(2) for t in tiles for m in range(MAPS)])
+
+        def sort_some(jobs):
+            for t, m, part in jobs:
+                sort_rows(t, m, part)
+                if part == 1 and m == MAPS - 1 and t + 3 < ROW_TILES:
+                    load(t + 3)
+
+        with tc.manual_schedule():
+            for t in range(3):
+                load(t)
+            sorted_first = MAPS * len(tiles_of(0))
+            sort_some(sort_jobs[:sorted_first])
+            grouped_of = {}
+            for s in range(len(steps) + LAG + FINISH_ROUNDS):
+                if s < len(steps):
+                    b, first, pairs, classes = steps[s]
+                    grouped_of[s] = group_step(pairs, transpose_step(pairs))
+                sort_some(
+                    sort_jobs[
+                        sorted_first + (SORTS_IN_TWO_ROUNDS * s + 1) // 2 : sorted_first + (SORTS_IN_TWO_ROUNDS * (s + 1) + 1) // 2
+                    ]
+                )
+                if 1 <= s <= len(steps):
+                    quantise_step(steps[s - 1][2], grouped_of[s - 1])
+                done = s - LAG
+                if done - 6 in last_step:
+                    total_up(last_step[done - 6])
+                if 0 <= done < len(steps):
+                    for g in steps[done][3]:
+                        multiply_class(steps[done][0], g)
+                if done in last_step:
+                    drain(last_step[done])
+                for o in range(OFFSETS):
+                    if done - 1 - o in last_step:
+                        square(last_step[done - 1 - o], o)
+                if done - 7 in last_step:
+                    scale_and_store(last_step[done - 7])

@@ -18,39 +18,42 @@ FLOPS = 2 * B * OFFSETS * C * C * K
 
 P = 128
 ROW_TILES = B * C // P
+REST = C - P
 CLASSES = 8
 ROW_BLOCKS = CLASSES + 1
 LEFT, MID, RIGHT = 0, 1, 2
 MAPS = 3
-BLOCK_COLS = MAPS * C
-N_MOVE = 512
-TAIL = C - P
-CODE_COLS = BLOCK_COLS * CLASSES + N_MOVE + P
-TAIL_COLS = (ROW_BLOCKS + 1) * TAIL
+BANK = 512
+LM = 0
+RM = LM + ROW_BLOCKS * 2 * P
+LR = RM + ROW_BLOCKS * P
+MR = LR + ROW_BLOCKS * 2 * REST
+EMPTY = MR + ROW_BLOCKS * REST
+FIRST_PAIR = EMPTY + REST
+CODE_COLS = FIRST_PAIR + 2 * REST
 SLOTS = 9
 SLOT_WORDS = 16
 SORTED_CLASSES = 4
 SORTED = 2 * SORTED_CLASSES * SLOTS * 2 * SLOT_WORDS
 PAD = 16
-BLOCK_ORDER = [1, 2, 3, 4, 5, 6, 7, 8, 0]
-FIRST_CLASS, LAST_CLASS = 1, 0
-SORTS_IN_TWO_ROUNDS = 3
 LAG = 2
-FINISH_ROUNDS = 8
+TOTAL, STORE = "total", "store"
+FINISH = [(0,), (1,), (2,), (3,), (4,), TOTAL, STORE]
+HASTY_FINISH = [(0, 1, 2), (3, 4), TOTAL, STORE]
+VECTOR_SQUARES = 3
 
 
-def tiles_of(b):
-    first = 3 * (b // 2)
-    return [first, first + 1] if b % 2 == 0 else [first + 2]
+def is_shared(t):
+    return t % 3 == 1
 
 
-def batch_pieces(t):
-    b, c0 = divmod(t * P, C)
-    rows = min(P, C - c0)
-    pieces = [(b, c0, 0, rows)]
-    if rows < P:
-        pieces.append((b + 1, 0, rows, P - rows))
-    return pieces
+def batches_of(t):
+    first = 2 * (t // 3)
+    return [first, first + 1] if is_shared(t) else [first + t % 3 // 2]
+
+
+def channels(b):
+    return (0, P) if b % 2 == 0 else (REST, 0)
 
 
 def tile_cofeature_fast_pa_kernel(tc, x, out):
@@ -60,7 +63,7 @@ def tile_cofeature_fast_pa_kernel(tc, x, out):
     with ExitStack() as ctx:
         const = ctx.enter_context(tc.tile_pool(name="const", bufs=1))
         sorted_pool = ctx.enter_context(tc.tile_pool(name="sorted", bufs=3))
-        stage_pool = ctx.enter_context(tc.tile_pool(name="stage", bufs=6))
+        stage_pool = ctx.enter_context(tc.tile_pool(name="stage", bufs=3))
         result_pool = ctx.enter_context(tc.tile_pool(name="result", bufs=2))
         small_pool = ctx.enter_context(tc.tile_pool(name="small", bufs=2))
         flip_pool = ctx.enter_context(tc.psum_pool(name="flip", bufs=4))
@@ -80,6 +83,10 @@ def tile_cofeature_fast_pa_kernel(tc, x, out):
         nc.vector.memset(warm[:], 1.0)
         nc.scalar.sqrt(out=warm[:], in_=warm[:])
         squares = const.tile([P, C], F32)
+        vector_squares = const.tile([P, C], F32)
+        inv_tiles = [const.tile([P, OFFSETS + MAPS], F32, name="inv%d" % i) for i in range(2)]
+        for inv in inv_tiles:
+            nc.vector.memset(inv[:], 1.0)
 
         plain_tiles = [const.tile([P, PAD + K + PAD], BF16, name="plain%d" % i) for i in range(3)]
         for plain in plain_tiles:
@@ -89,8 +96,6 @@ def tile_cofeature_fast_pa_kernel(tc, x, out):
         sorted_tiles = {}
         codes = {}
         scales = {}
-        tail_codes = {}
-        tail_scales = {}
         acc = {}
 
         def load(t):
@@ -126,180 +131,261 @@ def tile_cofeature_fast_pa_kernel(tc, x, out):
             start = ((u * SORTED_CLASSES + g_in_part) * SLOTS + first_slot) * SLOT_WORDS
             return sorted_tiles[(t, m, part)][:].bitcast(F32)[:, start : start + P]
 
-        used = BLOCK_COLS * CLASSES + 2 * C
         for i in range(3):
             code_tile = const.tile([P, CODE_COLS], U32, name="codes%d" % i, align_bytes=64)
             scale_tile = const.tile([P, CODE_COLS], U8, name="scales%d" % i, align_bytes=64)
-            nc.vector.memset(code_tile[:].bitcast(I32)[:, used:CODE_COLS], 0)
-            nc.vector.memset(scale_tile[:].bitcast(I32)[:, used // 4 : CODE_COLS // 4], 0)
-            tail_code_tile = const.tile([P, TAIL_COLS], U32, name="tail_codes%d" % i, align_bytes=64)
-            tail_scale_tile = const.tile([P, TAIL_COLS], U8, name="tail_scales%d" % i, align_bytes=64)
-            for first in (0, TAIL_COLS - TAIL):
-                nc.vector.memset(tail_code_tile[:].bitcast(I32)[:, first : first + TAIL], 0)
-                nc.vector.memset(tail_scale_tile[:].bitcast(I32)[:, first // 4 : (first + TAIL) // 4], 0)
+            nc.vector.memset(code_tile[:].bitcast(I32)[:, EMPTY : EMPTY + 2 * REST], 0)
+            nc.vector.memset(scale_tile[:].bitcast(I32)[:, EMPTY // 4 : (EMPTY + 2 * REST) // 4], 0)
             for b in range(i, B, 3):
                 codes[b], scales[b] = code_tile, scale_tile
-                tail_codes[b], tail_scales[b] = tail_code_tile, tail_scale_tile
 
-        def banks_of(pairs):
-            banks = [[(t, LEFT, h), (t, MID, h)] for t, h in pairs]
-            right = [(t, RIGHT, h) for t, h in pairs if h < CLASSES]
-            return banks + [right] if right else banks
+        def runs_of(step):
+            runs = []
+            for a, (t, h) in enumerate(step):
+                if runs and runs[-1][0] == t:
+                    runs[-1][1].append(h)
+                else:
+                    runs.append((t, [h], a))
+            return runs
 
-        def transpose_step(pairs):
-            flipped_banks = []
-            for units in banks_of(pairs):
-                flipped = flip_pool.tile([P, 4 * P], F32, tag="flip")
-                for a, (t, m, h) in enumerate(units):
-                    for u in range(2):
-                        at = (2 * a + u) * P
-                        nc.tensor.transpose(flipped[:, at : at + P], block_words(t, m, u, h), ident[:])
-                flipped_banks.append(flipped)
-            return flipped_banks
+        def is_needed(t, m, h):
+            return m != RIGHT or h < CLASSES or is_shared(t)
 
-        def group_step(pairs, flipped_banks):
-            grouped_tiles = []
-            for units, flipped in zip(banks_of(pairs), flipped_banks):
-                words = 2 * P * len(units)
-                grouped = stage_pool.tile([P, 8 * P], BF16, tag="grouped", align_bytes=64)
-                nc.scalar.copy(
-                    out=grouped[:].bitcast(F32)[:, 0:words].rearrange("p (a n u) -> p a n u", a=len(units), u=2),
-                    in_=flipped[:, 0:words].rearrange("p (a u n) -> p a n u", a=len(units), u=2),
-                )
-                grouped_tiles.append(grouped)
-            return grouped_tiles
+        def transpose_step(step):
+            banks = []
+            for m in range(MAPS):
+                bank = flip_pool.tile([P, BANK], F32, tag="flip")
+                for a, (t, h) in enumerate(step):
+                    if is_needed(t, m, h):
+                        for u in range(2):
+                            at = (2 * a + u) * P
+                            nc.tensor.transpose(bank[:, at : at + P], block_words(t, m, u, h), ident[:])
+                banks.append(bank)
+            return banks
 
-        def quantise_step(pairs, grouped_tiles):
-            for units, grouped in zip(banks_of(pairs), grouped_tiles):
-                for a, (t, m, h) in enumerate(units):
-                    for b, c0, n0, rows in batch_pieces(t):
-                        col = BLOCK_COLS * h + C * m + c0
-                        at = 4 * (P * a + n0)
-                        nc.vector.quantize_mx(
-                            out=codes[b][:, col : col + rows].bitcast(FP8X4),
-                            scales=scales[b][:, col : col + rows],
-                            in_=grouped[:, at : at + 4 * rows],
-                        )
-                        if m == MID and h >= 1 and c0 + rows == C:
-                            at = 4 * (P * a + n0 + rows - TAIL)
-                            nc.vector.quantize_mx(
-                                out=tail_codes[b][:, TAIL * h : TAIL * (h + 1)].bitcast(FP8X4),
-                                scales=tail_scales[b][:, TAIL * h : TAIL * (h + 1)],
-                                in_=grouped[:, at : at + 4 * TAIL],
+        def group_step(step, banks):
+            grouped = []
+            for t, blocks, a in runs_of(step):
+                wide = stage_pool.tile([P, 16 * P], BF16, tag="wide", align_bytes=64)
+                narrow = stage_pool.tile([P, 8 * P], BF16, tag="narrow", align_bytes=64)
+                grouped.append((wide, narrow))
+                for m, bank in enumerate(banks):
+                    count = len([h for h in blocks if is_needed(t, m, h)])
+                    words = 2 * P * count
+                    source = bank[:, 2 * P * a : 2 * P * a + words]
+                    narrow_map = MID if is_shared(t) else RIGHT
+                    if is_shared(t):
+                        source = source.rearrange("p (h u y n) -> p h y n u", h=count, u=2, y=2)
+                        if m == narrow_map:
+                            target = narrow[:].bitcast(F32)[:, 0:words].rearrange(
+                                "p (y h n u) -> p h y n u", y=2, h=count, u=2
                             )
+                        else:
+                            target = wide[:].bitcast(F32)[:, 0 : 2 * words].rearrange(
+                                "p (y h m n u) -> p m h y n u", y=2, h=count, m=2, u=2
+                            )[:, m // 2]
+                    else:
+                        source = source.rearrange("p (h u n) -> p h n u", h=count, u=2)
+                        if m == narrow_map:
+                            target = narrow[:].bitcast(F32)[:, 0:words].rearrange("p (h n u) -> p h n u", h=count, u=2)
+                        else:
+                            target = wide[:].bitcast(F32)[:, 0 : 2 * words].rearrange(
+                                "p (h m n u) -> p m h n u", h=count, m=2, u=2
+                            )[:, m]
+                    nc.scalar.copy(out=target, in_=source)
+            return grouped
 
-        def mx_pass(acc_tile, b, stationary, c_cols, d_cols, first, last):
-            stat_codes, stat_scales = stationary
+        def quantise(b, first, count, source):
+            nc.vector.quantize_mx(
+                out=codes[b][:, first : first + count].bitcast(FP8X4), scales=scales[b][:, first : first + count], in_=source
+            )
+
+        def quantise_step(step, grouped):
+            for (t, blocks, a), (wide, narrow) in zip(runs_of(step), grouped):
+                h, count = blocks[0], len(blocks)
+                if is_shared(t):
+                    for y, b in enumerate(batches_of(t)):
+                        words = 2 * REST * count
+                        quantise(b, LR + 2 * REST * h, words, wide[:, 4 * words * y : 4 * words * (y + 1)])
+                        words = REST * count
+                        quantise(b, MR + REST * h, words, narrow[:, 4 * words * y : 4 * words * (y + 1)])
+                        if h == 1:
+                            quantise(b, FIRST_PAIR + REST, REST, narrow[:, 4 * words * y : 4 * words * y + 4 * REST])
+                else:
+                    b = batches_of(t)[0]
+                    quantise(b, LM + 2 * P * h, 2 * P * count, wide[:, 0 : 8 * P * count])
+                    words = P * len([h for h in blocks if is_needed(t, RIGHT, h)])
+                    quantise(b, RM + P * h, words, narrow[:, 0 : 4 * words])
+
+        def mx_pass(acc_cols, b, c_first, d_first, first, last):
+            d_last = d_first + acc_cols.shape[1]
             nc.tensor.matmul_mx(
-                out=acc_tile,
-                lhsT=stat_codes[:, c_cols].bitcast(FP8X4),
-                lhsT_scale=stat_scales[:, c_cols],
-                rhs=codes[b][:, d_cols].bitcast(FP8X4),
-                rhs_scale=scales[b][:, d_cols],
+                out=acc_cols,
+                lhsT=codes[b][:, c_first : c_first + P].bitcast(FP8X4),
+                lhsT_scale=scales[b][:, c_first : c_first + P],
+                rhs=codes[b][:, d_first:d_last].bitcast(FP8X4),
+                rhs_scale=scales[b][:, d_first:d_last],
                 start=first,
                 stop=last,
             )
 
-        def multiply_class(b, g):
-            if g == FIRST_CLASS:
-                main0 = acc_pool.tile([P, N_MOVE], F32)
-                main1 = acc_pool.tile([P, N_MOVE], F32)
-                tail0 = acc_pool.tile([P, N_MOVE], F32)
-                tail1 = acc_pool.tile([P, N_MOVE], F32)
-                acc[b] = (main0, main1, tail0, tail1)
-            main0, main1, tail0, tail1 = acc[b]
-            c_first = BLOCK_COLS * (g + 1) + C * MID
-            d_first = BLOCK_COLS * g
-            for half, acc_tile in enumerate((main0, main1)):
-                mx_pass(
-                    acc_tile[:], b, (codes[b], scales[b]), slice(c_first, c_first + P),
-                    slice(d_first + N_MOVE * half, d_first + N_MOVE * (half + 1)), g == FIRST_CLASS, g == LAST_CLASS,
-                )
-            for h in [g] if g < CLASSES - 1 else [g, g + 1]:
-                c_cols = slice(TAIL * h, TAIL * h + P)
-                d_first = BLOCK_COLS * h
-                tail = (tail_codes[b], tail_scales[b])
-                first, last = h == FIRST_CLASS, h == LAST_CLASS
-                mx_pass(tail0[:], b, tail, c_cols, slice(d_first, d_first + N_MOVE), first, last)
-                mx_pass(tail1[:, 0:P], b, tail, c_cols, slice(d_first + N_MOVE, d_first + N_MOVE + P), first, last)
+        def multiply_main(b, g, first, last):
+            if first:
+                bank0 = acc_pool.tile([P, BANK], F32)
+                bank1 = acc_pool.tile([P, BANK], F32)
+                bank2 = acc_pool.tile([P, BANK], F32)
+                bank3 = acc_pool.tile([P, BANK], F32)
+                acc[b] = (bank0, bank1, bank2, bank3)
+            bank0, bank1 = acc[b][:2]
+            centre = LM + 2 * P * (g + 1) + P
+            mx_pass(bank0[:], b, centre, LM + 2 * P * g, first, last)
+            mx_pass(bank1[:, 0:P], b, centre, RM + P * g, first, False)
+            mx_pass(bank1[:, P : 3 * P], b, centre, LR + P * g, False, False)
+            mx_pass(bank1[:, 3 * P :], b, centre, MR + REST * g, False, last)
+
+        def multiply_rest(b, g, first, last):
+            bank2, bank3 = acc[b][2:]
+            windows = [g] if g < CLASSES - 1 else [g + 1, g]
+            for h in windows:
+                begin, end = first and h == windows[0], last and h == windows[-1]
+                centre = MR + REST * h if h > 0 else FIRST_PAIR
+                mx_pass(bank2[:, 0 : 2 * P], b, centre, LM + 2 * P * h, begin, False)
+                if h < CLASSES:
+                    mx_pass(bank2[:, 2 * P : 3 * P], b, centre, RM + P * h, False, False)
+                mx_pass(bank2[:, 3 * P :], b, centre, LR + P * h, False, end)
+                mx_pass(bank3[:, 0:P], b, centre, MR + REST * h, begin, end)
 
         result = {}
         sums = {}
-        inv = {}
 
         def drain(b):
-            main0, main1, tail0, tail1 = acc[b]
-            g_main = result_pool.tile([P, OFFSETS * C], F32, tag="g_main")
-            nc.vector.tensor_copy(out=g_main[:, 0:N_MOVE], in_=main0[:])
-            nc.vector.tensor_copy(out=g_main[:, N_MOVE:], in_=main1[:, 0 : OFFSETS * C - N_MOVE])
-            g_tail = result_pool.tile([P, MAPS * C], F32, tag="g_tail")
-            nc.scalar.copy(out=g_tail[:, 0:N_MOVE], in_=tail0[:])
-            nc.scalar.copy(out=g_tail[:, N_MOVE:], in_=tail1[:, 0 : MAPS * C - N_MOVE])
-            result[b] = (g_main, g_tail)
+            bank0, bank1, bank2, bank3 = acc[b]
+            a0, r0 = channels(b)
+            g_main = result_pool.tile([P, 2 * MAPS * C], F32, tag="g_main")
+            view = g_main[:].rearrange("p (i m d) -> p i m d", i=2, d=C)
+            nc.vector.tensor_copy(
+                out=view[:, :, 0:2, a0 : a0 + P], in_=bank0[:].rearrange("p (i m d) -> p i m d", i=2, m=2)
+            )
+            nc.vector.tensor_copy(out=view[:, 0, RIGHT, a0 : a0 + P], in_=bank1[:, 0:P])
+            nc.vector.tensor_copy(
+                out=view[:, :, LEFT : RIGHT + 1 : 2, r0 : r0 + REST],
+                in_=bank1[:, P : 3 * P].rearrange("p (i m d) -> p i m d", i=2, m=2),
+            )
+            nc.vector.tensor_copy(
+                out=view[:, :, MID, r0 : r0 + REST], in_=bank1[:, 3 * P :].rearrange("p (i d) -> p i d", i=2)
+            )
+            g_rest = result_pool.tile([P, MAPS * C], F32, tag="g_rest")
+            view = g_rest[:].rearrange("p (m d) -> p m d", d=C)
+            nc.scalar.copy(out=view[:, :, a0 : a0 + P], in_=bank2[:, 0 : 3 * P].rearrange("p (m d) -> p m d", m=MAPS))
+            nc.scalar.copy(
+                out=view[:, LEFT : RIGHT + 1 : 2, r0 : r0 + REST], in_=bank2[:, 3 * P :].rearrange("p (m d) -> p m d", m=2)
+            )
+            nc.scalar.copy(out=view[:, MID, r0 : r0 + REST], in_=bank3[:, 0:REST])
+            result[b] = (g_main, g_rest)
             sums_main = small_pool.tile([P, OFFSETS], F32, tag="sums_main")
-            sums_tail = small_pool.tile([P, MAPS], F32, tag="sums_tail")
-            sums[b] = (sums_main, sums_tail)
+            sums_rest = small_pool.tile([P, MAPS], F32, tag="sums_rest")
+            sums[b] = (sums_main, sums_rest)
+
+        def square_on_scalar(b, which, o):
+            nc.scalar.activation(
+                out=squares[:],
+                in_=result[b][which][:, C * o : C * (o + 1)],
+                func=mybir.ActivationFunctionType.Square,
+                accum_out=sums[b][which][:, o : o + 1],
+            )
 
         def square(b, o):
-            for g_sb, sums_sb in zip(result[b], sums[b]):
-                if C * o < g_sb.shape[1]:
-                    nc.scalar.activation(
-                        out=squares[:],
-                        in_=g_sb[:, C * o : C * (o + 1)],
-                        func=mybir.ActivationFunctionType.Square,
-                        accum_out=sums_sb[:, o : o + 1],
-                    )
+            square_on_scalar(b, 0, o)
+            if o < MAPS:
+                square_on_scalar(b, 1, o)
+
+        def square_at_once(b):
+            for o in range(VECTOR_SQUARES):
+                part = result[b][0][:, C * o : C * (o + 1)]
+                nc.vector.scalar_tensor_tensor(
+                    out=vector_squares[:], in0=part, scalar=1.0, in1=part,
+                    op0=mybir.AluOpType.mult, op1=mybir.AluOpType.mult, accum_out=sums[b][0][:, o : o + 1],
+                )
+            for m in range(MAPS):
+                square_on_scalar(b, 1, m)
+            for o in range(VECTOR_SQUARES, OFFSETS):
+                square_on_scalar(b, 0, o)
 
         def total_up(b):
-            sums_main, sums_tail = sums[b]
-            total = flip_pool.tile([P, 4 * P], F32, tag="flip")
+            sums_main, sums_rest = sums[b]
+            total = flip_pool.tile([P, BANK], F32, tag="flip")
             nc.tensor.matmul(out=total[:, 0:OFFSETS], lhsT=all_rows[:], rhs=sums_main[:], start=True, stop=False)
-            nc.tensor.matmul(out=total[:, 0:MAPS], lhsT=upper_rows[:], rhs=sums_tail[:], start=False, stop=False)
+            nc.tensor.matmul(out=total[:, 0:MAPS], lhsT=upper_rows[:], rhs=sums_rest[:], start=False, stop=False)
             nc.tensor.matmul(
-                out=total[:, MAPS:OFFSETS], lhsT=lower_rows[:], rhs=sums_tail[:, 0 : OFFSETS - MAPS], start=False, stop=True
+                out=total[:, MAPS:OFFSETS], lhsT=lower_rows[:], rhs=sums_rest[:, 0 : OFFSETS - MAPS], start=False, stop=True
             )
-            inv_tile = small_pool.tile([P, OFFSETS], F32, tag="inv")
-            nc.vector.tensor_scalar_max(out=inv_tile[:], in0=total[:, 0:OFFSETS], scalar1=EPS * EPS)
-            nc.scalar.sqrt(out=inv_tile[:], in_=inv_tile[:])
-            inv[b] = inv_tile
+            inv = inv_tiles[b % 2]
+            nc.scalar.sqrt(out=inv[:, 0:OFFSETS], in_=total[:, 0:OFFSETS])
+            nc.scalar.sqrt(out=inv[64:P, OFFSETS:], in_=total[64:P, 0:MAPS])
+            nc.scalar.sqrt(out=inv[0:64, OFFSETS : 2 * OFFSETS - MAPS], in_=total[0:64, MAPS:OFFSETS])
+            nc.vector.tensor_scalar_max(out=inv[:], in0=inv[:], scalar1=EPS)
+            nc.vector.reciprocal(out=inv[:], in_=inv[:])
 
         def scale_and_store(b):
-            g_main, g_tail = result[b]
-            nc.vector.reciprocal(out=inv[b][:], in_=inv[b][:])
+            g_main, g_rest = result[b]
+            inv = inv_tiles[b % 2]
+            a0, r0 = channels(b)
             by_channel = out[b].rearrange("o (c d) -> c o d", d=C)
-            main_view = g_main[:].rearrange("p (o d) -> p o d", d=C)
-            nc.vector.tensor_tensor(
-                out=main_view,
-                in0=main_view,
-                in1=inv[b][:].unsqueeze(2).to_broadcast([P, OFFSETS, C]),
-                op=mybir.AluOpType.mult,
-            )
-            nc.sync.dma_start(out=by_channel[0:P], in_=main_view)
-            for rows, first_o, last_o in ((slice(64, P), 0, MAPS), (slice(0, 64), MAPS, OFFSETS)):
-                tail_view = g_tail[rows, 0 : C * (last_o - first_o)].rearrange("p (o d) -> p o d", d=C)
-                nc.gpsimd.tensor_tensor(
-                    out=tail_view,
-                    in0=tail_view,
-                    in1=inv[b][rows, first_o:last_o].unsqueeze(2).to_broadcast([64, last_o - first_o, C]),
-                    op=mybir.AluOpType.mult,
+            for o in range(OFFSETS):
+                part = g_main[:, C * o : C * (o + 1)]
+                nc.vector.tensor_scalar_mul(out=part, in0=part, scalar1=inv[:, o : o + 1])
+            for m in range(MAPS):
+                part = g_rest[:, C * m : C * (m + 1)]
+                nc.scalar.activation(
+                    out=part, in_=part, func=mybir.ActivationFunctionType.Copy,
+                    scale=inv[:, OFFSETS + m : OFFSETS + m + 1],
                 )
-                nc.sync.dma_start(out=by_channel[P:C, first_o:last_o], in_=tail_view)
+            main_view = g_main[:, 0 : OFFSETS * C].rearrange("p (o d) -> p o d", d=C)
+            nc.sync.dma_start(out=by_channel[a0 : a0 + P], in_=main_view)
+            for rows, first_o, last_o in ((slice(64, P), 0, MAPS), (slice(0, 64), MAPS, OFFSETS)):
+                rest_view = g_rest[rows, 0 : C * (last_o - first_o)].rearrange("p (o d) -> p o d", d=C)
+                nc.sync.dma_start(out=by_channel[r0 : r0 + REST, first_o:last_o], in_=rest_view)
 
         steps = []
-        last_step = {}
-        sort_jobs = []
         for b in range(B):
-            tiles = tiles_of(b)
-            blocks_a_step = 2 // len(tiles)
-            for first in range(0, ROW_BLOCKS, blocks_a_step):
-                blocks = BLOCK_ORDER[first : first + blocks_a_step]
-                classes = [h - 1 for h in blocks if h >= 2] + [0 for h in blocks if h == 0]
-                steps.append((b, first, [(t, h) for h in blocks for t in tiles], classes))
-            last_step[len(steps) - 1] = b
-            sort_jobs.extend([(t, m, part) for part in range(2) for t in tiles for m in range(MAPS)])
+            tiles = [3 * (b // 2), 3 * (b // 2) + 1] if b % 2 == 0 else [3 * (b // 2) + 2]
+            steps.extend([[(t, h), (t, h + 1)] for h in (1, 3, 5, 7) for t in tiles])
+            steps.append([(t, 0) for t in tiles])
+        step_of = {unit: s for s, step in enumerate(steps) for unit in step}
+
+        waiting = []
+        for b in range(B):
+            own_tiles = [t for t in range(ROW_TILES) if b in batches_of(t)]
+            ready = [max(step_of[(t, h)] for t in own_tiles) for h in range(ROW_BLOCKS)]
+            waiting.extend(sorted((max(ready[g], ready[g + 1]) + LAG, b, g) for g in range(CLASSES)))
+        rounds = []
+        while waiting:
+            s = len(rounds)
+            b = waiting[0][1]
+            own = [job for job in waiting if job[1] == b]
+            now = [job for job in own if job[0] <= s]
+            if s < len(steps):
+                now = now[: 2 if len(now) > 2 or len(now) == len(own) or b == B - 1 else 1]
+            rounds.append([(b, g) for due, b, g in now])
+            waiting = [job for job in waiting if job not in now]
+        in_order = [job for now in rounds for job in now]
+        first_pass = {b: [job for job in in_order if job[0] == b][0] for b in range(B)}
+        last_pass = {b: [job for job in in_order if job[0] == b][-1] for b in range(B)}
+
+        finish = {}
+        for b in range(B - 1):
+            last_round = [s for s, now in enumerate(rounds) if last_pass[b] in now][0]
+            for i, part in enumerate(HASTY_FINISH if b == B - 2 else FINISH):
+                finish.setdefault(last_round + 1 + i, []).append((b, part))
+
+        sort_jobs = []
+        for t in range(ROW_TILES):
+            for part, first_block in ((0, 1), (1, 5)):
+                sort_jobs.extend([(step_of[(t, first_block)], t, m, part) for m in range(MAPS)])
+        sort_jobs = sorted(sort_jobs)
 
         def sort_some(jobs):
-            for t, m, part in jobs:
+            for first_step, t, m, part in jobs:
                 sort_rows(t, m, part)
                 if part == 1 and m == MAPS - 1 and t + 3 < ROW_TILES:
                     load(t + 3)
@@ -307,30 +393,34 @@ def tile_cofeature_fast_pa_kernel(tc, x, out):
         with tc.manual_schedule():
             for t in range(3):
                 load(t)
-            sorted_first = MAPS * len(tiles_of(0))
-            sort_some(sort_jobs[:sorted_first])
+            done = len([job for job in sort_jobs if job[0] <= 1])
+            sort_some(sort_jobs[:done])
             grouped_of = {}
-            for s in range(len(steps) + LAG + FINISH_ROUNDS):
+            for s in range(len(rounds)):
                 if s < len(steps):
-                    b, first, pairs, classes = steps[s]
-                    grouped_of[s] = group_step(pairs, transpose_step(pairs))
-                sort_some(
-                    sort_jobs[
-                        sorted_first + (SORTS_IN_TWO_ROUNDS * s + 1) // 2 : sorted_first + (SORTS_IN_TWO_ROUNDS * (s + 1) + 1) // 2
-                    ]
-                )
+                    grouped_of[s] = group_step(steps[s], transpose_step(steps[s]))
+                due = done
+                for i in range(done, len(sort_jobs)):
+                    rounds_left = max(1, sort_jobs[i][0] - s)
+                    due = max(due, done + (i + 1 - done + rounds_left - 1) // rounds_left)
+                sort_some(sort_jobs[done:due])
+                done = due
                 if 1 <= s <= len(steps):
-                    quantise_step(steps[s - 1][2], grouped_of[s - 1])
-                done = s - LAG
-                if done - 6 in last_step:
-                    total_up(last_step[done - 6])
-                if 0 <= done < len(steps):
-                    for g in steps[done][3]:
-                        multiply_class(steps[done][0], g)
-                if done in last_step:
-                    drain(last_step[done])
-                for o in range(OFFSETS):
-                    if done - 1 - o in last_step:
-                        square(last_step[done - 1 - o], o)
-                if done - 7 in last_step:
-                    scale_and_store(last_step[done - 7])
+                    quantise_step(steps[s - 1], grouped_of[s - 1])
+                for multiply in (multiply_main, multiply_rest):
+                    for b, g in rounds[s]:
+                        multiply(b, g, (b, g) == first_pass[b], (b, g) == last_pass[b])
+                for b in range(B):
+                    if last_pass[b] in rounds[s]:
+                        drain(b)
+                for b, part in finish.get(s, []):
+                    if part == TOTAL:
+                        total_up(b)
+                    elif part == STORE:
+                        scale_and_store(b)
+                    else:
+                        for o in part:
+                            square(b, o)
+            square_at_once(B - 1)
+            total_up(B - 1)
+            scale_and_store(B - 1)

@@ -23,6 +23,7 @@ CLASSES = 8
 ROW_BLOCKS = CLASSES + 1
 LEFT, MID, RIGHT = 0, 1, 2
 MAPS = 3
+MAP_ORDER = [MID, LEFT, RIGHT]
 BANK = 512
 LM = 0
 RM = LM + ROW_BLOCKS * 2 * P
@@ -32,10 +33,10 @@ EMPTY = MR + ROW_BLOCKS * REST
 FIRST_PAIR = EMPTY + REST
 CODE_COLS = FIRST_PAIR + 2 * REST
 SLOTS = 9
-SLOT_WORDS = 16
 SORTED_CLASSES = 4
-SORTED = 2 * SORTED_CLASSES * SLOTS * 2 * SLOT_WORDS
-PAD = 16
+SORTED = 2 * SORTED_CLASSES * SLOTS * W // 2
+FRONT = CLASSES * W + 16
+BACK = 16
 LAG = 2
 TOTAL, STORE = "total", "store"
 FINISH = [(0,), (1,), (2,), (3,), (4,), TOTAL, STORE]
@@ -88,10 +89,10 @@ def tile_cofeature_fast_pa_kernel(tc, x, out):
         for inv in inv_tiles:
             nc.vector.memset(inv[:], 1.0)
 
-        plain_tiles = [const.tile([P, PAD + K + PAD], BF16, name="plain%d" % i) for i in range(3)]
+        plain_tiles = [const.tile([P, FRONT + K + BACK], BF16, name="plain%d" % i) for i in range(3)]
         for plain in plain_tiles:
-            nc.vector.memset(plain[:, 0:PAD], 0.0)
-            nc.vector.memset(plain[:, PAD + K :], 0.0)
+            nc.vector.memset(plain[:, 0:FRONT], 0.0)
+            nc.vector.memset(plain[:, FRONT + K :], 0.0)
 
         sorted_tiles = {}
         codes = {}
@@ -99,36 +100,39 @@ def tile_cofeature_fast_pa_kernel(tc, x, out):
         acc = {}
 
         def load(t):
-            nc.sync.dma_start(out=plain_tiles[t % 3][:, PAD : PAD + K], in_=x_rows[t * P : (t + 1) * P, :])
-
-        def sort_rows(t, m, part):
             plain = plain_tiles[t % 3]
-            shift = m - MID
-            by_class = plain[:, PAD + shift : PAD + shift + K].rearrange(
-                "p (s g e u r) -> p g s e u r", s=8, g=CLASSES, e=2, u=2, r=16
+            rows = x_rows[t * P : (t + 1) * P, :]
+            nc.sync.dma_start(out=plain[:, FRONT : FRONT + K], in_=rows)
+            nc.sync.dma_start(out=plain[:, FRONT - W : FRONT], in_=rows[:, 0:W])
+
+        def by_class(t, shift, first, last):
+            start = FRONT - CLASSES * W + shift
+            rows = plain_tiles[t % 3][:, start : start + SLOTS * CLASSES * W]
+            return rows.rearrange("p (s g j) -> p g s j", s=SLOTS, g=CLASSES, j=W)[:, :, :, first:last]
+
+        def sorted_view(t, m, part):
+            return sorted_tiles[(t, m, part)][:].rearrange(
+                "p (u g s e r) -> p u g s e r", u=2, g=SORTED_CLASSES, s=SLOTS, e=2, r=16
             )
-            mine = slice(SORTED_CLASSES * part, SORTED_CLASSES * (part + 1))
+
+        def sort_map(t, m, part):
             tidy = sorted_pool.tile([P, SORTED], BF16, tag="sorted%d%d" % (m, part))
-            view = tidy[:].rearrange("p (u g s e r) -> p u g s e r", u=2, g=SORTED_CLASSES, s=SLOTS, e=2, r=16)
-            nc.vector.tensor_copy(
-                out=view[:, :, :, 1:SLOTS].rearrange("p u g s e r -> p g s e u r"), in_=by_class[:, mine]
-            )
-            edge = plain[:, PAD : PAD + K].rearrange("p (s g j) -> p g s j", s=8, g=CLASSES, j=W)
-            if m == LEFT:
-                nc.gpsimd.tensor_copy(out=view[:, 0, :, 1:SLOTS, 0, 0:1], in_=edge[:, mine, :, 0:1])
-            if m == RIGHT:
-                nc.gpsimd.tensor_copy(out=view[:, 1, :, 1:SLOTS, 1, 15:16], in_=edge[:, mine, :, W - 1 : W])
-            if part == 1:
-                first_part = sorted_tiles[(t, m, 0)][:].rearrange(
-                    "p (u g s e r) -> p u g s e r", u=2, g=SORTED_CLASSES, s=SLOTS, e=2, r=16
-                )
-                nc.gpsimd.tensor_copy(out=view[:, :, SORTED_CLASSES - 1, 0], in_=first_part[:, :, 0, 1])
             sorted_tiles[(t, m, part)] = tidy
+            mine = slice(SORTED_CLASSES * part, SORTED_CLASSES * (part + 1))
+            source = by_class(t, m - MID, 0, W)[:, mine].rearrange("p g s (e u r) -> p g s e u r", e=2, u=2)
+            nc.vector.tensor_copy(out=sorted_view(t, m, part).rearrange("p u g s e r -> p g s e u r"), in_=source)
+
+        def mend_borders(t, part):
+            mine = slice(SORTED_CLASSES * part, SORTED_CLASSES * (part + 1))
+            nc.vector.tensor_copy(out=sorted_view(t, LEFT, part)[:, 0, :, :, 0, 0:1], in_=by_class(t, 0, 0, 1)[:, mine])
+            nc.vector.tensor_copy(
+                out=sorted_view(t, RIGHT, part)[:, 1, :, :, 1, 15:16], in_=by_class(t, 0, W - 1, W)[:, mine]
+            )
 
         def block_words(t, m, u, h):
             g, first_slot = (CLASSES - 1, 0) if h == 0 else (h - 1, 1)
             part, g_in_part = divmod(g, SORTED_CLASSES)
-            start = ((u * SORTED_CLASSES + g_in_part) * SLOTS + first_slot) * SLOT_WORDS
+            start = ((u * SORTED_CLASSES + g_in_part) * SLOTS + first_slot) * W // 4
             return sorted_tiles[(t, m, part)][:].bitcast(F32)[:, start : start + P]
 
         for i in range(3):
@@ -153,7 +157,7 @@ def tile_cofeature_fast_pa_kernel(tc, x, out):
 
         def transpose_step(step):
             banks = []
-            for m in range(MAPS):
+            for m in MAP_ORDER:
                 bank = flip_pool.tile([P, BANK], F32, tag="flip")
                 for a, (t, h) in enumerate(step):
                     if is_needed(t, m, h):
@@ -169,7 +173,7 @@ def tile_cofeature_fast_pa_kernel(tc, x, out):
                 wide = stage_pool.tile([P, 16 * P], BF16, tag="wide", align_bytes=64)
                 narrow = stage_pool.tile([P, 8 * P], BF16, tag="narrow", align_bytes=64)
                 grouped.append((wide, narrow))
-                for m, bank in enumerate(banks):
+                for m, bank in zip(MAP_ORDER, banks):
                     count = len([h for h in blocks if is_needed(t, m, h)])
                     words = 2 * P * count
                     source = bank[:, 2 * P * a : 2 * P * a + words]
@@ -294,18 +298,21 @@ def tile_cofeature_fast_pa_kernel(tc, x, out):
                 accum_out=sums[b][which][:, o : o + 1],
             )
 
+        def square_on_vector(b, o):
+            part = result[b][0][:, C * o : C * (o + 1)]
+            nc.vector.scalar_tensor_tensor(
+                out=vector_squares[:], in0=part, scalar=1.0, in1=part,
+                op0=mybir.AluOpType.mult, op1=mybir.AluOpType.mult, accum_out=sums[b][0][:, o : o + 1],
+            )
+
         def square(b, o):
-            square_on_scalar(b, 0, o)
+            square_on_vector(b, o)
             if o < MAPS:
                 square_on_scalar(b, 1, o)
 
         def square_at_once(b):
             for o in range(VECTOR_SQUARES):
-                part = result[b][0][:, C * o : C * (o + 1)]
-                nc.vector.scalar_tensor_tensor(
-                    out=vector_squares[:], in0=part, scalar=1.0, in1=part,
-                    op0=mybir.AluOpType.mult, op1=mybir.AluOpType.mult, accum_out=sums[b][0][:, o : o + 1],
-                )
+                square_on_vector(b, o)
             for m in range(MAPS):
                 square_on_scalar(b, 1, m)
             for o in range(VECTOR_SQUARES, OFFSETS):
@@ -323,12 +330,12 @@ def tile_cofeature_fast_pa_kernel(tc, x, out):
             nc.scalar.sqrt(out=inv[:, 0:OFFSETS], in_=total[:, 0:OFFSETS])
             nc.scalar.sqrt(out=inv[64:P, OFFSETS:], in_=total[64:P, 0:MAPS])
             nc.scalar.sqrt(out=inv[0:64, OFFSETS : 2 * OFFSETS - MAPS], in_=total[0:64, MAPS:OFFSETS])
-            nc.vector.tensor_scalar_max(out=inv[:], in0=inv[:], scalar1=EPS)
-            nc.vector.reciprocal(out=inv[:], in_=inv[:])
 
         def scale_and_store(b):
             g_main, g_rest = result[b]
             inv = inv_tiles[b % 2]
+            nc.vector.tensor_scalar_max(out=inv[:], in0=inv[:], scalar1=EPS)
+            nc.vector.reciprocal(out=inv[:], in_=inv[:])
             a0, r0 = channels(b)
             by_channel = out[b].rearrange("o (c d) -> c o d", d=C)
             for o in range(OFFSETS):
@@ -365,7 +372,9 @@ def tile_cofeature_fast_pa_kernel(tc, x, out):
             own = [job for job in waiting if job[1] == b]
             now = [job for job in own if job[0] <= s]
             if s < len(steps):
-                now = now[: 2 if len(now) > 2 or len(now) == len(own) or b == B - 1 else 1]
+                now = now[:2]
+            else:
+                now = own
             rounds.append([(b, g) for due, b, g in now])
             waiting = [job for job in waiting if job not in now]
         in_order = [job for now in rounds for job in now]
@@ -380,15 +389,19 @@ def tile_cofeature_fast_pa_kernel(tc, x, out):
 
         sort_jobs = []
         for t in range(ROW_TILES):
-            for part, first_block in ((0, 1), (1, 5)):
-                sort_jobs.extend([(step_of[(t, first_block)], t, m, part) for m in range(MAPS)])
+            for part in range(2):
+                first_step = step_of[(t, SORTED_CLASSES * part + 1)]
+                sort_jobs.extend([(max(first_step - 1, min(first_step, 1)), t, part, i) for i in range(MAPS + 1)])
         sort_jobs = sorted(sort_jobs)
 
         def sort_some(jobs):
-            for first_step, t, m, part in jobs:
-                sort_rows(t, m, part)
-                if part == 1 and m == MAPS - 1 and t + 3 < ROW_TILES:
-                    load(t + 3)
+            for due, t, part, i in jobs:
+                if i < MAPS:
+                    sort_map(t, MAP_ORDER[i], part)
+                else:
+                    mend_borders(t, part)
+                    if part == 1 and t + 3 < ROW_TILES:
+                        load(t + 3)
 
         with tc.manual_schedule():
             for t in range(3):
@@ -410,9 +423,6 @@ def tile_cofeature_fast_pa_kernel(tc, x, out):
                 for multiply in (multiply_main, multiply_rest):
                     for b, g in rounds[s]:
                         multiply(b, g, (b, g) == first_pass[b], (b, g) == last_pass[b])
-                for b in range(B):
-                    if last_pass[b] in rounds[s]:
-                        drain(b)
                 for b, part in finish.get(s, []):
                     if part == TOTAL:
                         total_up(b)
@@ -421,6 +431,9 @@ def tile_cofeature_fast_pa_kernel(tc, x, out):
                     else:
                         for o in part:
                             square(b, o)
+                for b in range(B):
+                    if last_pass[b] in rounds[s]:
+                        drain(b)
             square_at_once(B - 1)
             total_up(B - 1)
             scale_and_store(B - 1)

@@ -38,10 +38,10 @@ SORTED = 2 * SORTED_CLASSES * SLOTS * W // 2
 FRONT = CLASSES * W + 16
 BACK = 16
 LAG = 2
-TOTAL, STORE = "total", "store"
-FINISH = [(0,), (1,), (2,), (3,), (4,), TOTAL, STORE]
-HASTY_FINISH = [(0, 1, 2), (3, 4), TOTAL, STORE]
-VECTOR_SQUARES = 3
+TOTAL, FLOOR, INVERT, STORE = "total", "floor", "invert", "store"
+FINISH = [((0,),), ((1,),), ((2,),), ((3,),), ((4,),), (TOTAL,), (FLOOR,), (INVERT,), (STORE,)]
+HASTY_FINISH = [((0, 1, 2),), ((3, 4),), (TOTAL,), (FLOOR, INVERT, STORE)]
+WASTE = 5
 
 
 def is_shared(t):
@@ -83,8 +83,8 @@ def tile_cofeature_fast_pa_kernel(tc, x, out):
         warm = const.tile([P, 1], F32)
         nc.vector.memset(warm[:], 1.0)
         nc.scalar.sqrt(out=warm[:], in_=warm[:])
-        squares = const.tile([P, C], F32)
-        vector_squares = const.tile([P, C], F32)
+        scalar_waste = const.tile([P, WASTE * C], F32)
+        vector_waste = const.tile([P, WASTE * C], F32)
         inv_tiles = [const.tile([P, OFFSETS + MAPS], F32, name="inv%d" % i) for i in range(2)]
         for inv in inv_tiles:
             nc.vector.memset(inv[:], 1.0)
@@ -105,34 +105,38 @@ def tile_cofeature_fast_pa_kernel(tc, x, out):
             nc.sync.dma_start(out=plain[:, FRONT : FRONT + K], in_=rows)
             nc.sync.dma_start(out=plain[:, FRONT - W : FRONT], in_=rows[:, 0:W])
 
-        def by_class(t, shift, first, last):
+        def by_class(t, shift, first, last, part):
             start = FRONT - CLASSES * W + shift
             rows = plain_tiles[t % 3][:, start : start + SLOTS * CLASSES * W]
-            return rows.rearrange("p (s g j) -> p g s j", s=SLOTS, g=CLASSES, j=W)[:, :, :, first:last]
+            mine = slice(SORTED_CLASSES * part, SORTED_CLASSES * (part + 1))
+            rows = rows.rearrange("p (s g j) -> p g s j", s=SLOTS, g=CLASSES, j=W)
+            return rows[:, mine, SLOTS - slots_of(part) :, first:last]
+
+        def slots_of(part):
+            return SLOTS if part == 1 else SLOTS - 1
 
         def sorted_view(t, m, part):
-            return sorted_tiles[(t, m, part)][:].rearrange(
-                "p (u g s e r) -> p u g s e r", u=2, g=SORTED_CLASSES, s=SLOTS, e=2, r=16
+            used = 2 * SORTED_CLASSES * slots_of(part) * W // 2
+            return sorted_tiles[(t, m, part)][:, 0:used].rearrange(
+                "p (u g s e r) -> p u g s e r", u=2, g=SORTED_CLASSES, s=slots_of(part), e=2, r=16
             )
 
         def sort_map(t, m, part):
             tidy = sorted_pool.tile([P, SORTED], BF16, tag="sorted%d%d" % (m, part))
             sorted_tiles[(t, m, part)] = tidy
-            mine = slice(SORTED_CLASSES * part, SORTED_CLASSES * (part + 1))
-            source = by_class(t, m - MID, 0, W)[:, mine].rearrange("p g s (e u r) -> p g s e u r", e=2, u=2)
+            source = by_class(t, m - MID, 0, W, part).rearrange("p g s (e u r) -> p g s e u r", e=2, u=2)
             nc.vector.tensor_copy(out=sorted_view(t, m, part).rearrange("p u g s e r -> p g s e u r"), in_=source)
 
         def mend_borders(t, part):
-            mine = slice(SORTED_CLASSES * part, SORTED_CLASSES * (part + 1))
-            nc.vector.tensor_copy(out=sorted_view(t, LEFT, part)[:, 0, :, :, 0, 0:1], in_=by_class(t, 0, 0, 1)[:, mine])
+            nc.vector.tensor_copy(out=sorted_view(t, LEFT, part)[:, 0, :, :, 0, 0:1], in_=by_class(t, 0, 0, 1, part))
             nc.vector.tensor_copy(
-                out=sorted_view(t, RIGHT, part)[:, 1, :, :, 1, 15:16], in_=by_class(t, 0, W - 1, W)[:, mine]
+                out=sorted_view(t, RIGHT, part)[:, 1, :, :, 1, 15:16], in_=by_class(t, 0, W - 1, W, part)
             )
 
         def block_words(t, m, u, h):
-            g, first_slot = (CLASSES - 1, 0) if h == 0 else (h - 1, 1)
-            part, g_in_part = divmod(g, SORTED_CLASSES)
-            start = ((u * SORTED_CLASSES + g_in_part) * SLOTS + first_slot) * W // 4
+            part, g_in_part = divmod(CLASSES - 1 if h == 0 else h - 1, SORTED_CLASSES)
+            first_slot = 0 if h == 0 else slots_of(part) - CLASSES
+            start = ((u * SORTED_CLASSES + g_in_part) * slots_of(part) + first_slot) * W // 4
             return sorted_tiles[(t, m, part)][:].bitcast(F32)[:, start : start + P]
 
         for i in range(3):
@@ -290,33 +294,25 @@ def tile_cofeature_fast_pa_kernel(tc, x, out):
             sums_rest = small_pool.tile([P, MAPS], F32, tag="sums_rest")
             sums[b] = (sums_main, sums_rest)
 
-        def square_on_scalar(b, which, o):
+        def square_on_scalar(b, o):
             nc.scalar.activation(
-                out=squares[:],
-                in_=result[b][which][:, C * o : C * (o + 1)],
+                out=scalar_waste[:, C * o : C * (o + 1)],
+                in_=result[b][1][:, C * o : C * (o + 1)],
                 func=mybir.ActivationFunctionType.Square,
-                accum_out=sums[b][which][:, o : o + 1],
+                accum_out=sums[b][1][:, o : o + 1],
             )
 
         def square_on_vector(b, o):
             part = result[b][0][:, C * o : C * (o + 1)]
             nc.vector.scalar_tensor_tensor(
-                out=vector_squares[:], in0=part, scalar=1.0, in1=part,
+                out=vector_waste[:, C * o : C * (o + 1)], in0=part, scalar=1.0, in1=part,
                 op0=mybir.AluOpType.mult, op1=mybir.AluOpType.mult, accum_out=sums[b][0][:, o : o + 1],
             )
 
         def square(b, o):
             square_on_vector(b, o)
             if o < MAPS:
-                square_on_scalar(b, 1, o)
-
-        def square_at_once(b):
-            for o in range(VECTOR_SQUARES):
-                square_on_vector(b, o)
-            for m in range(MAPS):
-                square_on_scalar(b, 1, m)
-            for o in range(VECTOR_SQUARES, OFFSETS):
-                square_on_scalar(b, 0, o)
+                square_on_scalar(b, o)
 
         def total_up(b):
             sums_main, sums_rest = sums[b]
@@ -331,11 +327,15 @@ def tile_cofeature_fast_pa_kernel(tc, x, out):
             nc.scalar.sqrt(out=inv[64:P, OFFSETS:], in_=total[64:P, 0:MAPS])
             nc.scalar.sqrt(out=inv[0:64, OFFSETS : 2 * OFFSETS - MAPS], in_=total[0:64, MAPS:OFFSETS])
 
+        def floor_norms(b):
+            nc.vector.tensor_scalar_max(out=inv_tiles[b % 2][:], in0=inv_tiles[b % 2][:], scalar1=EPS)
+
+        def invert_norms(b):
+            nc.vector.reciprocal(out=inv_tiles[b % 2][:], in_=inv_tiles[b % 2][:])
+
         def scale_and_store(b):
             g_main, g_rest = result[b]
             inv = inv_tiles[b % 2]
-            nc.vector.tensor_scalar_max(out=inv[:], in0=inv[:], scalar1=EPS)
-            nc.vector.reciprocal(out=inv[:], in_=inv[:])
             a0, r0 = channels(b)
             by_channel = out[b].rearrange("o (c d) -> c o d", d=C)
             for o in range(OFFSETS):
@@ -372,7 +372,7 @@ def tile_cofeature_fast_pa_kernel(tc, x, out):
             own = [job for job in waiting if job[1] == b]
             now = [job for job in own if job[0] <= s]
             if s < len(steps):
-                now = now[:2]
+                now = now[: 2 if len(now) > 2 or len(now) == len(own) or b == B - 1 else 1]
             else:
                 now = own
             rounds.append([(b, g) for due, b, g in now])
@@ -384,8 +384,8 @@ def tile_cofeature_fast_pa_kernel(tc, x, out):
         finish = {}
         for b in range(B - 1):
             last_round = [s for s, now in enumerate(rounds) if last_pass[b] in now][0]
-            for i, part in enumerate(HASTY_FINISH if b == B - 2 else FINISH):
-                finish.setdefault(last_round + 1 + i, []).append((b, part))
+            for i, parts in enumerate(HASTY_FINISH if b == B - 2 else FINISH):
+                finish.setdefault(last_round + 1 + i, []).extend([(b, part) for part in parts])
 
         sort_jobs = []
         for t in range(ROW_TILES):
@@ -412,12 +412,6 @@ def tile_cofeature_fast_pa_kernel(tc, x, out):
             for s in range(len(rounds)):
                 if s < len(steps):
                     grouped_of[s] = group_step(steps[s], transpose_step(steps[s]))
-                due = done
-                for i in range(done, len(sort_jobs)):
-                    rounds_left = max(1, sort_jobs[i][0] - s)
-                    due = max(due, done + (i + 1 - done + rounds_left - 1) // rounds_left)
-                sort_some(sort_jobs[done:due])
-                done = due
                 if 1 <= s <= len(steps):
                     quantise_step(steps[s - 1], grouped_of[s - 1])
                 for multiply in (multiply_main, multiply_rest):
@@ -426,14 +420,27 @@ def tile_cofeature_fast_pa_kernel(tc, x, out):
                 for b, part in finish.get(s, []):
                     if part == TOTAL:
                         total_up(b)
+                    elif part == FLOOR:
+                        floor_norms(b)
+                    elif part == INVERT:
+                        invert_norms(b)
                     elif part == STORE:
                         scale_and_store(b)
                     else:
                         for o in part:
                             square(b, o)
+                due = done
+                for i in range(done, len(sort_jobs)):
+                    rounds_left = max(1, sort_jobs[i][0] - s)
+                    due = max(due, done + (i + 1 - done + rounds_left - 1) // rounds_left)
+                sort_some(sort_jobs[done:due])
+                done = due
                 for b in range(B):
                     if last_pass[b] in rounds[s]:
                         drain(b)
-            square_at_once(B - 1)
+            for o in range(OFFSETS):
+                square(B - 1, o)
             total_up(B - 1)
+            floor_norms(B - 1)
+            invert_norms(B - 1)
             scale_and_store(B - 1)

@@ -24,6 +24,7 @@ ROW_BLOCKS = CLASSES + 1
 LEFT, MID, RIGHT = 0, 1, 2
 MAPS = 3
 MAP_ORDER = [MID, LEFT, RIGHT]
+MEND_ORDER = [LEFT, RIGHT, MID]
 BANK = 512
 LM = 0
 RM = LM + ROW_BLOCKS * 2 * P
@@ -39,7 +40,7 @@ FRONT = CLASSES * W + 16
 BACK = 16
 LAG = 2
 TOTAL, FLOOR, INVERT, STORE = "total", "floor", "invert", "store"
-FINISH = [((0,),), ((1,),), ((2,),), ((3,),), ((4,),), (TOTAL,), (FLOOR,), (INVERT,), (STORE,)]
+FINISH = [((0,),), ((1,),), ((2,),), ((3, 4),), (TOTAL,), (FLOOR,), (INVERT,), (STORE,)]
 HASTY_FINISH = [((0, 1, 2),), ((3, 4),), (TOTAL,), (FLOOR, INVERT, STORE)]
 WASTE = 5
 
@@ -64,7 +65,7 @@ def tile_cofeature_fast_pa_kernel(tc, x, out):
     with ExitStack() as ctx:
         const = ctx.enter_context(tc.tile_pool(name="const", bufs=1))
         sorted_pool = ctx.enter_context(tc.tile_pool(name="sorted", bufs=3))
-        stage_pool = ctx.enter_context(tc.tile_pool(name="stage", bufs=3))
+        stage_pool = ctx.enter_context(tc.tile_pool(name="stage", bufs=4))
         result_pool = ctx.enter_context(tc.tile_pool(name="result", bufs=2))
         small_pool = ctx.enter_context(tc.tile_pool(name="small", bufs=2))
         flip_pool = ctx.enter_context(tc.psum_pool(name="flip", bufs=4))
@@ -142,8 +143,9 @@ def tile_cofeature_fast_pa_kernel(tc, x, out):
         for i in range(3):
             code_tile = const.tile([P, CODE_COLS], U32, name="codes%d" % i, align_bytes=64)
             scale_tile = const.tile([P, CODE_COLS], U8, name="scales%d" % i, align_bytes=64)
-            nc.vector.memset(code_tile[:].bitcast(I32)[:, EMPTY : EMPTY + 2 * REST], 0)
-            nc.vector.memset(scale_tile[:].bitcast(I32)[:, EMPTY // 4 : (EMPTY + 2 * REST) // 4], 0)
+            for first, last in ((MR - REST, MR), (EMPTY, EMPTY + 2 * REST)):
+                nc.vector.memset(code_tile[:].bitcast(I32)[:, first:last], 0)
+                nc.vector.memset(scale_tile[:].bitcast(I32)[:, first // 4 : last // 4], 0)
             for b in range(i, B, 3):
                 codes[b], scales[b] = code_tile, scale_tile
 
@@ -156,15 +158,15 @@ def tile_cofeature_fast_pa_kernel(tc, x, out):
                     runs.append((t, [h], a))
             return runs
 
-        def is_needed(t, m, h):
-            return m != RIGHT or h < CLASSES or is_shared(t)
+        def is_needed(m, h):
+            return m != RIGHT or h < CLASSES
 
         def transpose_step(step):
             banks = []
             for m in MAP_ORDER:
                 bank = flip_pool.tile([P, BANK], F32, tag="flip")
                 for a, (t, h) in enumerate(step):
-                    if is_needed(t, m, h):
+                    if is_needed(m, h):
                         for u in range(2):
                             at = (2 * a + u) * P
                             nc.tensor.transpose(bank[:, at : at + P], block_words(t, m, u, h), ident[:])
@@ -178,7 +180,8 @@ def tile_cofeature_fast_pa_kernel(tc, x, out):
                 narrow = stage_pool.tile([P, 8 * P], BF16, tag="narrow", align_bytes=64)
                 grouped.append((wide, narrow))
                 for m, bank in zip(MAP_ORDER, banks):
-                    count = len([h for h in blocks if is_needed(t, m, h)])
+                    count = len([h for h in blocks if is_needed(m, h)])
+                    wide_words = 4 * P * len(blocks)
                     words = 2 * P * count
                     source = bank[:, 2 * P * a : 2 * P * a + words]
                     narrow_map = MID if is_shared(t) else RIGHT
@@ -189,15 +192,15 @@ def tile_cofeature_fast_pa_kernel(tc, x, out):
                                 "p (y h n u) -> p h y n u", y=2, h=count, u=2
                             )
                         else:
-                            target = wide[:].bitcast(F32)[:, 0 : 2 * words].rearrange(
-                                "p (y h m n u) -> p m h y n u", y=2, h=count, m=2, u=2
-                            )[:, m // 2]
+                            target = wide[:].bitcast(F32)[:, 0:wide_words].rearrange(
+                                "p (y h m n u) -> p m h y n u", y=2, h=len(blocks), m=2, u=2
+                            )[:, m // 2, 0:count]
                     else:
                         source = source.rearrange("p (h u n) -> p h n u", h=count, u=2)
                         if m == narrow_map:
                             target = narrow[:].bitcast(F32)[:, 0:words].rearrange("p (h n u) -> p h n u", h=count, u=2)
                         else:
-                            target = wide[:].bitcast(F32)[:, 0 : 2 * words].rearrange(
+                            target = wide[:].bitcast(F32)[:, 0:wide_words].rearrange(
                                 "p (h m n u) -> p m h n u", h=count, m=2, u=2
                             )[:, m]
                     nc.scalar.copy(out=target, in_=source)
@@ -213,8 +216,12 @@ def tile_cofeature_fast_pa_kernel(tc, x, out):
                 h, count = blocks[0], len(blocks)
                 if is_shared(t):
                     for y, b in enumerate(batches_of(t)):
-                        words = 2 * REST * count
-                        quantise(b, LR + 2 * REST * h, words, wide[:, 4 * words * y : 4 * words * (y + 1)])
+                        at = 8 * REST * count * y
+                        full = len([h for h in blocks if is_needed(RIGHT, h)])
+                        quantise(b, LR + 2 * REST * h, 2 * REST * full, wide[:, at : at + 8 * REST * full])
+                        if full < count:
+                            at += 8 * REST * full
+                            quantise(b, LR + 2 * REST * (h + full), REST, wide[:, at : at + 4 * REST])
                         words = REST * count
                         quantise(b, MR + REST * h, words, narrow[:, 4 * words * y : 4 * words * (y + 1)])
                         if h == 1:
@@ -222,7 +229,7 @@ def tile_cofeature_fast_pa_kernel(tc, x, out):
                 else:
                     b = batches_of(t)[0]
                     quantise(b, LM + 2 * P * h, 2 * P * count, wide[:, 0 : 8 * P * count])
-                    words = P * len([h for h in blocks if is_needed(t, RIGHT, h)])
+                    words = P * len([h for h in blocks if is_needed(RIGHT, h)])
                     quantise(b, RM + P * h, words, narrow[:, 0 : 4 * words])
 
         def mx_pass(acc_cols, b, c_first, d_first, first, last):
@@ -244,9 +251,11 @@ def tile_cofeature_fast_pa_kernel(tc, x, out):
                 bank2 = acc_pool.tile([P, BANK], F32)
                 bank3 = acc_pool.tile([P, BANK], F32)
                 acc[b] = (bank0, bank1, bank2, bank3)
-            bank0, bank1 = acc[b][:2]
+            mx_pass(acc[b][0][:], b, LM + 2 * P * (g + 1) + P, LM + 2 * P * g, first, last)
+
+        def multiply_mixed(b, g, first, last):
+            bank1 = acc[b][1]
             centre = LM + 2 * P * (g + 1) + P
-            mx_pass(bank0[:], b, centre, LM + 2 * P * g, first, last)
             mx_pass(bank1[:, 0:P], b, centre, RM + P * g, first, False)
             mx_pass(bank1[:, P : 3 * P], b, centre, LR + P * g, False, False)
             mx_pass(bank1[:, 3 * P :], b, centre, MR + REST * g, False, last)
@@ -302,15 +311,16 @@ def tile_cofeature_fast_pa_kernel(tc, x, out):
                 accum_out=sums[b][1][:, o : o + 1],
             )
 
-        def square_on_vector(b, o):
-            part = result[b][0][:, C * o : C * (o + 1)]
+        def square_on_vector(b, which, o):
+            part = result[b][which][:, C * o : C * (o + 1)]
+            place = C * ((o + OFFSETS * which) % WASTE)
             nc.vector.scalar_tensor_tensor(
-                out=vector_waste[:, C * o : C * (o + 1)], in0=part, scalar=1.0, in1=part,
-                op0=mybir.AluOpType.mult, op1=mybir.AluOpType.mult, accum_out=sums[b][0][:, o : o + 1],
+                out=vector_waste[:, place : place + C], in0=part, scalar=1.0, in1=part,
+                op0=mybir.AluOpType.mult, op1=mybir.AluOpType.mult, accum_out=sums[b][which][:, o : o + 1],
             )
 
         def square(b, o):
-            square_on_vector(b, o)
+            square_on_vector(b, 0, o)
             if o < MAPS:
                 square_on_scalar(b, o)
 
@@ -372,7 +382,7 @@ def tile_cofeature_fast_pa_kernel(tc, x, out):
             own = [job for job in waiting if job[1] == b]
             now = [job for job in own if job[0] <= s]
             if s < len(steps):
-                now = now[: 2 if len(now) > 2 or len(now) == len(own) or b == B - 1 else 1]
+                now = now[: 2 if len(now) > 3 or b == B - 1 or b == B - 2 and len(now) == len(own) else 1]
             else:
                 now = own
             rounds.append([(b, g) for due, b, g in now])
@@ -397,7 +407,7 @@ def tile_cofeature_fast_pa_kernel(tc, x, out):
         def sort_some(jobs):
             for due, t, part, i in jobs:
                 if i < MAPS:
-                    sort_map(t, MAP_ORDER[i], part)
+                    sort_map(t, (MAP_ORDER if due < 2 else MEND_ORDER)[i], part)
                 else:
                     mend_borders(t, part)
                     if part == 1 and t + 3 < ROW_TILES:
@@ -414,7 +424,7 @@ def tile_cofeature_fast_pa_kernel(tc, x, out):
                     grouped_of[s] = group_step(steps[s], transpose_step(steps[s]))
                 if 1 <= s <= len(steps):
                     quantise_step(steps[s - 1], grouped_of[s - 1])
-                for multiply in (multiply_main, multiply_rest):
+                for multiply in (multiply_main, multiply_mixed, multiply_rest):
                     for b, g in rounds[s]:
                         multiply(b, g, (b, g) == first_pass[b], (b, g) == last_pass[b])
                 for b, part in finish.get(s, []):
@@ -439,7 +449,10 @@ def tile_cofeature_fast_pa_kernel(tc, x, out):
                     if last_pass[b] in rounds[s]:
                         drain(b)
             for o in range(OFFSETS):
-                square(B - 1, o)
+                square_on_vector(B - 1, 0, o)
+            square_on_vector(B - 1, 1, 0)
+            for o in range(1, MAPS):
+                square_on_scalar(B - 1, o)
             total_up(B - 1)
             floor_norms(B - 1)
             invert_norms(B - 1)

from contextlib import ExitStack

import concourse.mybir as mybir
from concourse.masks import make_identity

F32 = mybir.dt.float32
BF16 = mybir.dt.bfloat16
U32 = mybir.dt.uint32
I32 = mybir.dt.int32
U8 = mybir.dt.uint8
FP8X4 = mybir.dt.float8_e4m3fn_x4

B, C, H, W = 4, 192, 64, 64
K = H * W
OFFSETS = 5
EPS = 1e-12
FLOPS = 2 * B * OFFSETS * C * C * K

P = 128
ROW_TILES = B * C // P
REST = C - P
CLASSES = 8
ROW_BLOCKS = CLASSES + 1
LEFT, MID, RIGHT = 0, 1, 2
MAPS = 3
MAP_ORDER = [MID, LEFT, RIGHT]
MEND_ORDER = [LEFT, RIGHT, MID]
BANK = 512
LM = 0
RM = LM + ROW_BLOCKS * 2 * P
LR = RM + ROW_BLOCKS * P
MR = LR + ROW_BLOCKS * 2 * REST
EMPTY = MR + ROW_BLOCKS * REST
FIRST_PAIR = EMPTY + REST
CODE_COLS = FIRST_PAIR + 2 * REST
SLOTS = 9
SORTED_CLASSES = 4
SORTED = 2 * SORTED_CLASSES * SLOTS * W // 2
FRONT = CLASSES * W + 16
BACK = 16
LAG = 2
TOTAL, FLOOR, INVERT, STORE = "total", "floor", "invert", "store"
FINISH = [((0,),), ((1,),), ((2,),), ((3, 4),), (TOTAL,), (FLOOR,), (INVERT,), (STORE,)]
HASTY_FINISH = [((0, 1, 2),), ((3, 4),), (TOTAL,), (FLOOR, INVERT, STORE)]
WASTE = 5


def is_shared(t):
    return t % 3 == 1


def batches_of(t):
    first = 2 * (t // 3)
    return [first, first + 1] if is_shared(t) else [first + t % 3 // 2]


def channels(b):
    return (0, P) if b % 2 == 0 else (REST, 0)


def tile_cofeature_fast_pa_kernel(tc, x, out):
    nc = tc.nc
    x_rows = x.rearrange("b c i j -> (b c) (i j)")

    with ExitStack() as ctx:
        const = ctx.enter_context(tc.tile_pool(name="const", bufs=1))
        sorted_pool = ctx.enter_context(tc.tile_pool(name="sorted", bufs=3))
        stage_pool = ctx.enter_context(tc.tile_pool(name="stage", bufs=4))
        result_pool = ctx.enter_context(tc.tile_pool(name="result", bufs=2))
        small_pool = ctx.enter_context(tc.tile_pool(name="small", bufs=2))
        flip_pool = ctx.enter_context(tc.psum_pool(name="flip", bufs=4))
        acc_pool = ctx.enter_context(tc.psum_pool(name="acc", bufs=1))

        ident = const.tile([P, P], F32)
        make_identity(nc, ident[:])
        all_rows = const.tile([P, P], F32)
        nc.vector.memset(all_rows[:], 1.0)
        upper_rows = const.tile([P, P], F32)
        nc.vector.memset(upper_rows[0:64, :], 0.0)
        nc.vector.memset(upper_rows[64:P, :], 1.0)
        lower_rows = const.tile([P, P], F32)
        nc.vector.memset(lower_rows[0:64, :], 1.0)
        nc.vector.memset(lower_rows[64:P, :], 0.0)
        warm = const.tile([P, 1], F32)
        nc.vector.memset(warm[:], 1.0)
        nc.scalar.sqrt(out=warm[:], in_=warm[:])
        scalar_waste = const.tile([P, WASTE * C], F32)
        vector_waste = const.tile([P, WASTE * C], F32)
        inv_tiles = [const.tile([P, OFFSETS + MAPS], F32, name="inv%d" % i) for i in range(2)]
        for inv in inv_tiles:
            nc.vector.memset(inv[:], 1.0)

        plain_tiles = [const.tile([P, FRONT + K + BACK], BF16, name="plain%d" % i) for i in range(3)]
        for plain in plain_tiles:
            nc.vector.memset(plain[:, 0:FRONT], 0.0)
            nc.vector.memset(plain[:, FRONT + K :], 0.0)

        sorted_tiles = {}
        codes = {}
        scales = {}
        acc = {}

        def load(t):
            plain = plain_tiles[t % 3]
            rows = x_rows[t * P : (t + 1) * P, :]
            nc.sync.dma_start(out=plain[:, FRONT : FRONT + K], in_=rows)
            nc.sync.dma_start(out=plain[:, FRONT - W : FRONT], in_=rows[:, 0:W])

        def by_class(t, shift, first, last, part):
            start = FRONT - CLASSES * W + shift
            rows = plain_tiles[t % 3][:, start : start + SLOTS * CLASSES * W]
            mine = slice(SORTED_CLASSES * part, SORTED_CLASSES * (part + 1))
            rows = rows.rearrange("p (s g j) -> p g s j", s=SLOTS, g=CLASSES, j=W)
            return rows[:, mine, SLOTS - slots_of(part) :, first:last]

        def slots_of(part):
            return SLOTS if part == 1 else SLOTS - 1

        def sorted_view(t, m, part):
            used = 2 * SORTED_CLASSES * slots_of(part) * W // 2
            return sorted_tiles[(t, m, part)][:, 0:used].rearrange(
                "p (u g s e r) -> p u g s e r", u=2, g=SORTED_CLASSES, s=slots_of(part), e=2, r=16
            )

        def sort_map(t, m, part):
            tidy = sorted_pool.tile([P, SORTED], BF16, tag="sorted%d%d" % (m, part))
            sorted_tiles[(t, m, part)] = tidy
            source = by_class(t, m - MID, 0, W, part).rearrange("p g s (e u r) -> p g s e u r", e=2, u=2)
            nc.vector.tensor_copy(out=sorted_view(t, m, part).rearrange("p u g s e r -> p g s e u r"), in_=source)

        def mend_borders(t, part):
            nc.vector.tensor_copy(out=sorted_view(t, LEFT, part)[:, 0, :, :, 0, 0:1], in_=by_class(t, 0, 0, 1, part))
            nc.vector.tensor_copy(
                out=sorted_view(t, RIGHT, part)[:, 1, :, :, 1, 15:16], in_=by_class(t, 0, W - 1, W, part)
            )

        def block_words(t, m, u, h):
            part, g_in_part = divmod(CLASSES - 1 if h == 0 else h - 1, SORTED_CLASSES)
            first_slot = 0 if h == 0 else slots_of(part) - CLASSES
            start = ((u * SORTED_CLASSES + g_in_part) * slots_of(part) + first_slot) * W // 4
            return sorted_tiles[(t, m, part)][:].bitcast(F32)[:, start : start + P]

        for i in range(3):
            code_tile = const.tile([P, CODE_COLS], U32, name="codes%d" % i, align_bytes=64)
            scale_tile = const.tile([P, CODE_COLS], U8, name="scales%d" % i, align_bytes=64)
            for first, last in ((MR - REST, MR), (EMPTY, EMPTY + 2 * REST)):
                nc.vector.memset(code_tile[:].bitcast(I32)[:, first:last], 0)
                nc.vector.memset(scale_tile[:].bitcast(I32)[:, first // 4 : last // 4], 0)
            for b in range(i, B, 3):
                codes[b], scales[b] = code_tile, scale_tile

        def runs_of(step):
            runs = []
            for a, (t, h) in enumerate(step):
                if runs and runs[-1][0] == t:
                    runs[-1][1].append(h)
                else:
                    runs.append((t, [h], a))
            return runs

        def is_needed(m, h):
            return m != RIGHT or h < CLASSES

        def transpose_step(step):
            banks = []
            for m in MAP_ORDER:
                bank = flip_pool.tile([P, BANK], F32, tag="flip")
                for a, (t, h) in enumerate(step):
                    if is_needed(m, h):
                        for u in range(2):
                            at = (2 * a + u) * P
                            nc.tensor.transpose(bank[:, at : at + P], block_words(t, m, u, h), ident[:])
                banks.append(bank)
            return banks

        def group_step(step, banks):
            grouped = []
            for t, blocks, a in runs_of(step):
                wide = stage_pool.tile([P, 16 * P], BF16, tag="wide", align_bytes=64)
                narrow = stage_pool.tile([P, 8 * P], BF16, tag="narrow", align_bytes=64)
                grouped.append((wide, narrow))
                for m, bank in zip(MAP_ORDER, banks):
                    count = len([h for h in blocks if is_needed(m, h)])
                    wide_words = 4 * P * len(blocks)
                    words = 2 * P * count
                    source = bank[:, 2 * P * a : 2 * P * a + words]
                    narrow_map = MID if is_shared(t) else RIGHT
                    if is_shared(t):
                        source = source.rearrange("p (h u y n) -> p h y n u", h=count, u=2, y=2)
                        if m == narrow_map:
                            target = narrow[:].bitcast(F32)[:, 0:words].rearrange(
                                "p (y h n u) -> p h y n u", y=2, h=count, u=2
                            )
                        else:
                            target = wide[:].bitcast(F32)[:, 0:wide_words].rearrange(
                                "p (y h m n u) -> p m h y n u", y=2, h=len(blocks), m=2, u=2
                            )[:, m // 2, 0:count]
                    else:
                        source = source.rearrange("p (h u n) -> p h n u", h=count, u=2)
                        if m == narrow_map:
                            target = narrow[:].bitcast(F32)[:, 0:words].rearrange("p (h n u) -> p h n u", h=count, u=2)
                        else:
                            target = wide[:].bitcast(F32)[:, 0:wide_words].rearrange(
                                "p (h m n u) -> p m h n u", h=count, m=2, u=2
                            )[:, m]
                    nc.scalar.copy(out=target, in_=source)
            return grouped

        def quantise(b, first, count, source):
            nc.vector.quantize_mx(
                out=codes[b][:, first : first + count].bitcast(FP8X4), scales=scales[b][:, first : first + count], in_=source
            )

        def quantise_step(step, grouped):
            for (t, blocks, a), (wide, narrow) in zip(runs_of(step), grouped):
                h, count = blocks[0], len(blocks)
                if is_shared(t):
                    for y, b in enumerate(batches_of(t)):
                        at = 8 * REST * count * y
                        full = len([h for h in blocks if is_needed(RIGHT, h)])
                        quantise(b, LR + 2 * REST * h, 2 * REST * full, wide[:, at : at + 8 * REST * full])
                        if full < count:
                            at += 8 * REST * full
                            quantise(b, LR + 2 * REST * (h + full), REST, wide[:, at : at + 4 * REST])
                        words = REST * count
                        quantise(b, MR + REST * h, words, narrow[:, 4 * words * y : 4 * words * (y + 1)])
                        if h == 1:
                            quantise(b, FIRST_PAIR + REST, REST, narrow[:, 4 * words * y : 4 * words * y + 4 * REST])
                else:
                    b = batches_of(t)[0]
                    quantise(b, LM + 2 * P * h, 2 * P * count, wide[:, 0 : 8 * P * count])
                    words = P * len([h for h in blocks if is_needed(RIGHT, h)])
                    quantise(b, RM + P * h, words, narrow[:, 0 : 4 * words])

        def mx_pass(acc_cols, b, c_first, d_first, first, last):
            d_last = d_first + acc_cols.shape[1]
            nc.tensor.matmul_mx(
                out=acc_cols,
                lhsT=codes[b][:, c_first : c_first + P].bitcast(FP8X4),
                lhsT_scale=scales[b][:, c_first : c_first + P],
                rhs=codes[b][:, d_first:d_last].bitcast(FP8X4),
                rhs_scale=scales[b][:, d_first:d_last],
                start=first,
                stop=last,
            )

        def multiply_main(b, g, first, last):
            if first:
                bank0 = acc_pool.tile([P, BANK], F32)
                bank1 = acc_pool.tile([P, BANK], F32)
                bank2 = acc_pool.tile([P, BANK], F32)
                bank3 = acc_pool.tile([P, BANK], F32)
                acc[b] = (bank0, bank1, bank2, bank3)
            mx_pass(acc[b][0][:], b, LM + 2 * P * (g + 1) + P, LM + 2 * P * g, first, last)

        def multiply_mixed(b, g, first, last):
            bank1 = acc[b][1]
            centre = LM + 2 * P * (g + 1) + P
            mx_pass(bank1[:, 0:P], b, centre, RM + P * g, first, False)
            mx_pass(bank1[:, P : 3 * P], b, centre, LR + P * g, False, False)
            mx_pass(bank1[:, 3 * P :], b, centre, MR + REST * g, False, last)

        def multiply_rest(b, g, first, last):
            bank2, bank3 = acc[b][2:]
            windows = [g] if g < CLASSES - 1 else [g + 1, g]
            for h in windows:
                begin, end = first and h == windows[0], last and h == windows[-1]
                centre = MR + REST * h if h > 0 else FIRST_PAIR
                mx_pass(bank2[:, 0 : 2 * P], b, centre, LM + 2 * P * h, begin, False)
                if h < CLASSES:
                    mx_pass(bank2[:, 2 * P : 3 * P], b, centre, RM + P * h, False, False)
                mx_pass(bank2[:, 3 * P :], b, centre, LR + P * h, False, end)
                mx_pass(bank3[:, 0:P], b, centre, MR + REST * h, begin, end)

        result = {}
        sums = {}

        def drain(b):
            bank0, bank1, bank2, bank3 = acc[b]
            a0, r0 = channels(b)
            g_main = result_pool.tile([P, 2 * MAPS * C], F32, tag="g_main")
            view = g_main[:].rearrange("p (i m d) -> p i m d", i=2, d=C)
            nc.vector.tensor_copy(
                out=view[:, :, 0:2, a0 : a0 + P], in_=bank0[:].rearrange("p (i m d) -> p i m d", i=2, m=2)
            )
            nc.vector.tensor_copy(out=view[:, 0, RIGHT, a0 : a0 + P], in_=bank1[:, 0:P])
            nc.vector.tensor_copy(
                out=view[:, :, LEFT : RIGHT + 1 : 2, r0 : r0 + REST],
                in_=bank1[:, P : 3 * P].rearrange("p (i m d) -> p i m d", i=2, m=2),
            )
            nc.vector.tensor_copy(
                out=view[:, :, MID, r0 : r0 + REST], in_=bank1[:, 3 * P :].rearrange("p (i d) -> p i d", i=2)
            )
            g_rest = result_pool.tile([P, MAPS * C], F32, tag="g_rest")
            view = g_rest[:].rearrange("p (m d) -> p m d", d=C)
            nc.scalar.copy(out=view[:, :, a0 : a0 + P], in_=bank2[:, 0 : 3 * P].rearrange("p (m d) -> p m d", m=MAPS))
            nc.scalar.copy(
                out=view[:, LEFT : RIGHT + 1 : 2, r0 : r0 + REST], in_=bank2[:, 3 * P :].rearrange("p (m d) -> p m d", m=2)
            )
            nc.scalar.copy(out=view[:, MID, r0 : r0 + REST], in_=bank3[:, 0:REST])
            result[b] = (g_main, g_rest)
            sums_main = small_pool.tile([P, OFFSETS], F32, tag="sums_main")
            sums_rest = small_pool.tile([P, MAPS], F32, tag="sums_rest")
            sums[b] = (sums_main, sums_rest)

        def square_on_scalar(b, o):
            nc.scalar.activation(
                out=scalar_waste[:, C * o : C * (o + 1)],
                in_=result[b][1][:, C * o : C * (o + 1)],
                func=mybir.ActivationFunctionType.Square,
                accum_out=sums[b][1][:, o : o + 1],
            )

        def square_on_vector(b, which, o):
            part = result[b][which][:, C * o : C * (o + 1)]
            place = C * ((o + OFFSETS * which) % WASTE)
            nc.vector.scalar_tensor_tensor(
                out=vector_waste[:, place : place + C], in0=part, scalar=1.0, in1=part,
                op0=mybir.AluOpType.mult, op1=mybir.AluOpType.mult, accum_out=sums[b][which][:, o : o + 1],
            )

        def square(b, o):
            square_on_vector(b, 0, o)
            if o < MAPS:
                square_on_scalar(b, o)

        def total_up(b):
            sums_main, sums_rest = sums[b]
            total = flip_pool.tile([P, BANK], F32, tag="flip")
            nc.tensor.matmul(out=total[:, 0:OFFSETS], lhsT=all_rows[:], rhs=sums_main[:], start=True, stop=False)
            nc.tensor.matmul(out=total[:, 0:MAPS], lhsT=upper_rows[:], rhs=sums_rest[:], start=False, stop=False)
            nc.tensor.matmul(
                out=total[:, MAPS:OFFSETS], lhsT=lower_rows[:], rhs=sums_rest[:, 0 : OFFSETS - MAPS], start=False, stop=True
            )
            inv = inv_tiles[b % 2]
            nc.scalar.sqrt(out=inv[:, 0:OFFSETS], in_=total[:, 0:OFFSETS])
            nc.scalar.sqrt(out=inv[64:P, OFFSETS:], in_=total[64:P, 0:MAPS])
            nc.scalar.sqrt(out=inv[0:64, OFFSETS : 2 * OFFSETS - MAPS], in_=total[0:64, MAPS:OFFSETS])

        def floor_norms(b):
            nc.vector.tensor_scalar_max(out=inv_tiles[b % 2][:], in0=inv_tiles[b % 2][:], scalar1=EPS)

        def invert_norms(b):
            nc.vector.reciprocal(out=inv_tiles[b % 2][:], in_=inv_tiles[b % 2][:])

        def scale_and_store(b):
            g_main, g_rest = result[b]
            inv = inv_tiles[b % 2]
            a0, r0 = channels(b)
            by_channel = out[b].rearrange("o (c d) -> c o d", d=C)
            for o in range(OFFSETS):
                part = g_main[:, C * o : C * (o + 1)]
                nc.vector.tensor_scalar_mul(out=part, in0=part, scalar1=inv[:, o : o + 1])
            for m in range(MAPS):
                part = g_rest[:, C * m : C * (m + 1)]
                nc.scalar.activation(
                    out=part, in_=part, func=mybir.ActivationFunctionType.Copy,
                    scale=inv[:, OFFSETS + m : OFFSETS + m + 1],
                )
            main_view = g_main[:, 0 : OFFSETS * C].rearrange("p (o d) -> p o d", d=C)
            nc.sync.dma_start(out=by_channel[a0 : a0 + P], in_=main_view)
            for rows, first_o, last_o in ((slice(64, P), 0, MAPS), (slice(0, 64), MAPS, OFFSETS)):
                rest_view = g_rest[rows, 0 : C * (last_o - first_o)].rearrange("p (o d) -> p o d", d=C)
                nc.sync.dma_start(out=by_channel[r0 : r0 + REST, first_o:last_o], in_=rest_view)

        steps = []
        for b in range(B):
            tiles = [3 * (b // 2), 3 * (b // 2) + 1] if b % 2 == 0 else [3 * (b // 2) + 2]
            steps.extend([[(t, h), (t, h + 1)] for h in (1, 3, 5, 7) for t in tiles])
            steps.append([(t, 0) for t in tiles])
        step_of = {unit: s for s, step in enumerate(steps) for unit in step}

        waiting = []
        for b in range(B):
            own_tiles = [t for t in range(ROW_TILES) if b in batches_of(t)]
            ready = [max(step_of[(t, h)] for t in own_tiles) for h in range(ROW_BLOCKS)]
            waiting.extend(sorted((max(ready[g], ready[g + 1]) + LAG, b, g) for g in range(CLASSES)))
        rounds = []
        while waiting:
            s = len(rounds)
            b = waiting[0][1]
            own = [job for job in waiting if job[1] == b]
            now = [job for job in own if job[0] <= s]
            if s < len(steps):
                now = now[: 2 if len(now) > 3 or b == B - 1 or b == B - 2 and len(now) == len(own) else 1]
            else:
                now = own
            rounds.append([(b, g) for due, b, g in now])
            waiting = [job for job in waiting if job not in now]
        in_order = [job for now in rounds for job in now]
        first_pass = {b: [job for job in in_order if job[0] == b][0] for b in range(B)}
        last_pass = {b: [job for job in in_order if job[0] == b][-1] for b in range(B)}

        finish = {}
        for b in range(B - 1):
            last_round = [s for s, now in enumerate(rounds) if last_pass[b] in now][0]
            for i, parts in enumerate(HASTY_FINISH if b == B - 2 else FINISH):
                finish.setdefault(last_round + 1 + i, []).extend([(b, part) for part in parts])

        sort_jobs = []
        for t in range(ROW_TILES):
            for part in range(2):
                first_step = step_of[(t, SORTED_CLASSES * part + 1)]
                sort_jobs.extend([(max(first_step - 1, min(first_step, 1)), t, part, i) for i in range(MAPS + 1)])
        sort_jobs = sorted(sort_jobs)

        def sort_some(jobs):
            for due, t, part, i in jobs:
                if i < MAPS:
                    sort_map(t, (MAP_ORDER if due < 2 else MEND_ORDER)[i], part)
                else:
                    mend_borders(t, part)
                    if part == 1 and t + 3 < ROW_TILES:
                        load(t + 3)

        with tc.manual_schedule():
            for t in range(3):
                load(t)
            done = len([job for job in sort_jobs if job[0] <= 1])
            sort_some(sort_jobs[:done])
            grouped_of = {}
            for s in range(len(rounds)):
                if s < len(steps):
                    grouped_of[s] = group_step(steps[s], transpose_step(steps[s]))
                if 1 <= s <= len(steps):
                    quantise_step(steps[s - 1], grouped_of[s - 1])
                for multiply in (multiply_main, multiply_mixed, multiply_rest):
                    for b, g in rounds[s]:
                        multiply(b, g, (b, g) == first_pass[b], (b, g) == last_pass[b])
                for b, part in finish.get(s, []):
                    if part == TOTAL:
                        total_up(b)
                    elif part == FLOOR:
                        floor_norms(b)
                    elif part == INVERT:
                        invert_norms(b)
                    elif part == STORE:
                        scale_and_store(b)
                    else:
                        for o in part:
                            square(b, o)
                due = done
                for i in range(done, len(sort_jobs)):
                    rounds_left = max(1, sort_jobs[i][0] - s)
                    due = max(due, done + (i + 1 - done + rounds_left - 1) // rounds_left)
                sort_some(sort_jobs[done:due])
                done = due
                for b in range(B):
                    if last_pass[b] in rounds[s]:
                        drain(b)
            for o in range(OFFSETS):
                square_on_vector(B - 1, 0, o)
            square_on_vector(B - 1, 1, 0)
            for o in range(1, MAPS):
                square_on_scalar(B - 1, o)
            total_up(B - 1)
            floor_norms(B - 1)
            invert_norms(B - 1)
            scale_and_store(B - 1)
